import numpy as np
import ml_dtypes


def mxq(x, axis, fmt="e4m3"):
    dtype, down = {"e4m3": (ml_dtypes.float8_e4m3fn, 7), "e5m2": (ml_dtypes.float8_e5m2, 14)}[fmt]
    v = np.moveaxis(np.asarray(x, np.float32).astype(ml_dtypes.bfloat16).astype(np.float64), axis, -1)
    blocks = v.reshape(v.shape[:-1] + (-1, 32))
    amax = np.abs(blocks).max(-1, keepdims=True)
    byte = np.maximum(np.where(amax > 0, np.frexp(amax)[1] - 1 + 127, 0) - down, 1)
    scale = np.exp2(byte - 127.0)
    codes = (blocks / scale).astype(np.float32).astype(dtype).astype(np.float64)
    return np.moveaxis((codes * scale).reshape(v.shape), -1, axis)


WIDE = False


def mx_kscale(k):
    if not WIDE:
        return np.ones(k)
    levels = np.array([10, -10, 5, -5, 0])
    a = np.random.permutation(np.resize(levels, k // 512 * 4)).reshape(k // 512, 4)
    idx = np.arange(k)
    return np.exp2(a[idx // 512, idx % 128 // 32])


BF16 = ml_dtypes.bfloat16


def bf(x):
    return np.asarray(x, np.float32).astype(BF16)


def f64(x):
    return np.asarray(x).astype(np.float64)


B, GRID, PATCH, D, NH, NCLS = 128, 3, 16, 1024, 16, 1000
N = GRID * GRID + 1
D3 = 3 * D
EPS = 1e-5


def layernorm(v, g, b):
    mu = v.mean(-1, keepdims=True)
    var = ((v - mu) ** 2).mean(-1, keepdims=True)
    return (v - mu) / np.sqrt(var + EPS) * g + b


def setup_inputs():
    s = mx_kscale(D)
    return {
        "attn_l": bf(np.random.standard_normal((B, N, D)) * s),
        "wo_l": bf(np.random.standard_normal((D, D)) / np.sqrt(D) / s),
        "bo_l": bf(np.random.standard_normal(D) * 0.1),
        "g1": bf(1.0 + np.random.standard_normal(D) * 0.1),
        "be1": bf(np.random.standard_normal(D) * 0.1),
        "wqkv_g": bf(np.random.standard_normal((D3, D)) / np.sqrt(D)),
        "bqkv_g": bf(np.random.standard_normal(D3) * 0.1),
    }


def reference(attn_l, wo_l, bo_l, g1, be1, wqkv_g, bqkv_g):
    y = (mxq(f64(attn_l), 2, "e4m3") @ mxq(f64(wo_l), 1, "e4m3").T) + f64(bo_l)
    local = layernorm(y, f64(g1), f64(be1))
    return (mxq(local, 2, "e4m3") @ mxq(f64(wqkv_g), 1, "e4m3").T) + f64(bqkv_g)

@@ -1,0 +1,272 @@
+from contextlib import ExitStack
+
+import concourse.mybir as mybir
+from concourse.masks import make_identity
+
+F32 = mybir.dt.float32
+BF16 = mybir.dt.bfloat16
+U32 = mybir.dt.uint32
+U8 = mybir.dt.uint8
+FP8X4 = mybir.dt.float8_e4m3fn_x4
+ALU = mybir.AluOpType
+ACT = mybir.ActivationFunctionType
+
+P = 128
+TOKEN_TILES = 10
+D = 1024
+D3 = 3072
+EPS = 1e-5
+PACK = 4
+K_PASS = P * PACK
+PASSES = D // K_PASS
+PAIRS = 2
+WORDS_PER_PASS = K_PASS // PAIRS
+CHUNK = 512
+ROW_TILES = CHUNK // P
+STORE_CHUNKS = 3
+
+FLOPS = 2 * P * TOKEN_TILES * D * (D + D3)
+
+
+def copy_bank(nc, on_vector, out, in_):
+    if on_vector:
+        nc.vector.tensor_copy(out=out, in_=in_)
+    else:
+        nc.scalar.copy(out=out, in_=in_)
+
+
+def quantise_weight_chunk(nc, stage, psum_t, ident, row_tiles, codes, scales, share_with_vector):
+    for g in range(PASSES):
+        grouped = stage.tile([P, PACK * CHUNK], BF16, align_bytes=64, tag="w_grouped")
+        grouped_words = grouped[:].bitcast(F32).rearrange("q (n u) -> q n u", u=PAIRS)
+        for half in range(2):
+            bank = psum_t.tile([P, PAIRS, 2, P], F32, tag="tp")
+            for u in range(PAIRS):
+                first = WORDS_PER_PASS * g + P * u
+                for j in range(2):
+                    nc.tensor.transpose(
+                        bank[:, u, j, :], row_tiles[2 * half + j][:, first : first + P], ident[:]
+                    )
+            copy_bank(
+                nc,
+                share_with_vector and half == 1,
+                out=grouped_words[:, 2 * P * half : 2 * P * (half + 1), :],
+                in_=bank[:].rearrange("q u j r -> q (j r) u"),
+            )
+        nc.vector.quantize_mx(
+            out=codes[:, g, :].bitcast(FP8X4), scales=scales[:, g, :], in_=grouped[:]
+        )
+
+
+def tile_hlgan_pb_kernel(tc, attn_l, wo_l, bo_l, g1, be1, wqkv_g, bqkv_g, out):
+    nc = tc.nc
+    with ExitStack() as ctx:
+        const = ctx.enter_context(tc.tile_pool(name="const", bufs=1))
+        keep = ctx.enter_context(tc.tile_pool(name="keep", bufs=1))
+        raw = ctx.enter_context(tc.tile_pool(name="raw", bufs=1))
+        stage = ctx.enter_context(tc.tile_pool(name="stage", bufs=2))
+        norm = ctx.enter_context(tc.tile_pool(name="norm", bufs=2))
+        small = ctx.enter_context(tc.tile_pool(name="small", bufs=4))
+        out_pool = ctx.enter_context(tc.tile_pool(name="out_pool", bufs=4))
+        psum_t = ctx.enter_context(tc.psum_pool(name="psum_t", bufs=3))
+        psum_acc = ctx.enter_context(tc.psum_pool(name="psum_acc", bufs=5))
+
+        ident = const.tile([P, P], F32)
+        make_identity(nc, ident[:])
+        eps = const.tile([P, 1], F32)
+        nc.vector.memset(eps[:], EPS)
+        warm = const.tile([P, 1], F32)
+        nc.scalar.activation(out=warm[:], in_=eps[:], func=ACT.Sqrt)
+
+        x_codes = keep.tile([P, TOKEN_TILES, PASSES, P], U32, align_bytes=64)
+        x_scales = keep.tile([P, TOKEN_TILES, PASSES, P], U8, align_bytes=64)
+        wo_codes = keep.tile([P, PASSES, D], U32, align_bytes=64)
+        wo_scales = keep.tile([P, PASSES, D], U8, align_bytes=64)
+        local_codes = keep.tile([P, TOKEN_TILES, PASSES, P], U32, align_bytes=64)
+        local_scales = keep.tile([P, TOKEN_TILES, PASSES, P], U8, align_bytes=64)
+        wqkv_codes = keep.tile([P, PASSES, D3], U32, align_bytes=64)
+        wqkv_scales = keep.tile([P, PASSES, D3], U8, align_bytes=64)
+        wqkv_raw = keep.tile([P, D3 // P, D], BF16)
+
+        bo_rows = const.tile([P, D], BF16)
+        nc.scalar.dma_start(out=bo_rows[:], in_=bo_l.partition_broadcast(P))
+        g_raw = const.tile([P, D // P], BF16)
+        nc.scalar.dma_start(
+            out=g_raw[:].rearrange("q (a e) -> q a e", e=PAIRS),
+            in_=g1.rearrange("(a q e) -> q a e", q=P, e=PAIRS),
+        )
+        be_raw = const.tile([P, D // P], BF16)
+        nc.scalar.dma_start(
+            out=be_raw[:].rearrange("q (a e) -> q a e", e=PAIRS),
+            in_=be1.rearrange("(a q e) -> q a e", q=P, e=PAIRS),
+        )
+        bo_cols = const.tile([P, D], BF16)
+        nc.vector.tensor_copy(
+            out=bo_cols[:].rearrange("p (a e q) -> p a e q", e=PAIRS, q=P),
+            in_=bo_rows[:].rearrange("p (a q e) -> p a e q", q=P, e=PAIRS),
+        )
+        gain = const.tile([P, D // P], F32)
+        nc.vector.tensor_copy(out=gain[:], in_=g_raw[:])
+        shift = const.tile([P, D // P], F32)
+        nc.vector.tensor_copy(out=shift[:], in_=be_raw[:])
+
+        wo_raw = raw.tile([P, D // (PAIRS * P), PAIRS, D], BF16)
+        wo_view = wo_l.rearrange("(a q e) k -> q a e k", q=P, e=PAIRS)
+        for a in range(0, D // (PAIRS * P), 2):
+            nc.sync.dma_start(out=wo_raw[:, a : a + 2], in_=wo_view[:, a : a + 2])
+        x_raw = raw.tile([P, TOKEN_TILES, D], BF16)
+        for i in range(0, TOKEN_TILES, 2):
+            nc.sync.dma_start(out=x_raw[:, i : i + 2, :], in_=attn_l[:, i : i + 2, :])
+        for n in range(D3 // CHUNK):
+            nc.sync.dma_start(
+                out=wqkv_raw[:, ROW_TILES * n : ROW_TILES * (n + 1), :],
+                in_=wqkv_g[CHUNK * n : CHUNK * (n + 1), :].rearrange("(j p) k -> p j k", p=P),
+            )
+        bqkv_rows = const.tile([P, D3], BF16)
+        nc.sync.dma_start(out=bqkv_rows[:], in_=bqkv_g.partition_broadcast(P))
+
+        for h in range(D // CHUNK):
+            cols = slice(CHUNK * h, CHUNK * (h + 1))
+            quantise_weight_chunk(
+                nc,
+                stage,
+                psum_t,
+                ident,
+                [wo_raw[:, 2 * h + j // 2, j % 2, :].bitcast(F32) for j in range(ROW_TILES)],
+                wo_codes[:, :, cols],
+                wo_scales[:, :, cols],
+                True,
+            )
+        for i in range(TOKEN_TILES):
+            x_words = x_raw[:, i, :].bitcast(F32)
+            bank = psum_t.tile([P, PASSES, PAIRS, P], F32, tag="tp")
+            for g in range(PASSES):
+                for u in range(PAIRS):
+                    first = WORDS_PER_PASS * g + P * u
+                    nc.tensor.transpose(bank[:, g, u, :], x_words[:, first : first + P], ident[:])
+            x_grouped = stage.tile([P, D], BF16, align_bytes=64)
+            copy_bank(
+                nc,
+                i % 2 == 1,
+                out=x_grouped[:].bitcast(F32).rearrange("q (g r u) -> q g r u", g=PASSES, u=PAIRS),
+                in_=bank[:].rearrange("q g u r -> q g r u"),
+            )
+            nc.vector.quantize_mx(
+                out=x_codes[:, i].rearrange("q g r -> q (g r)").bitcast(FP8X4),
+                scales=x_scales[:, i].rearrange("q g r -> q (g r)"),
+                in_=x_grouped[:],
+            )
+
+        for n in range(D3 // CHUNK):
+            cols = slice(CHUNK * n, CHUNK * (n + 1))
+            quantise_weight_chunk(
+                nc,
+                stage,
+                psum_t,
+                ident,
+                [wqkv_raw[:, ROW_TILES * n + j, :].bitcast(F32) for j in range(ROW_TILES)],
+                wqkv_codes[:, :, cols],
+                wqkv_scales[:, :, cols],
+                False,
+            )
+
+        for i in range(TOKEN_TILES):
+            y = norm.tile([P, D], F32, bufs=3)
+            y_sum = small.tile([P, D // CHUNK], F32)
+            for h in range(D // CHUNK):
+                cols = slice(CHUNK * h, CHUNK * (h + 1))
+                acc = psum_acc.tile([P, CHUNK], F32, tag="acc")
+                for g in range(PASSES):
+                    nc.tensor.matmul_mx(
+                        out=acc[:],
+                        lhsT=x_codes[:, i, g, :].bitcast(FP8X4),
+                        lhsT_scale=x_scales[:, i, g, :],
+                        rhs=wo_codes[:, g, cols].bitcast(FP8X4),
+                        rhs_scale=wo_scales[:, g, cols],
+                        start=(g == 0),
+                        stop=(g == PASSES - 1),
+                    )
+                nc.vector.scalar_tensor_tensor(
+                    out=y[:, cols],
+                    in0=acc[:],
+                    scalar=0.0,
+                    in1=bo_cols[:, cols],
+                    op0=ALU.add,
+                    op1=ALU.add,
+                    accum_out=y_sum[:, h : h + 1],
+                )
+            neg_mean = small.tile([P, 1], F32)
+            nc.vector.tensor_scalar(
+                out=neg_mean[:],
+                in0=y_sum[:, 0:1],
+                scalar1=y_sum[:, 1:2],
+                scalar2=-1.0 / D,
+                op0=ALU.add,
+                op1=ALU.mult,
+            )
+            squares = norm.tile([P, D], BF16)
+            sum_sq = small.tile([P, 1], F32)
+            nc.scalar.activation(
+                out=squares[:], in_=y[:], func=ACT.Square, bias=neg_mean[:], accum_out=sum_sq[:]
+            )
+            std = small.tile([P, 1], F32)
+            nc.scalar.activation(out=std[:], in_=sum_sq[:], func=ACT.Sqrt, bias=eps[:], scale=1.0 / D)
+            rstd = small.tile([P, 1], F32)
+            nc.vector.reciprocal(out=rstd[:], in_=std[:])
+            neg_mean_rstd = small.tile([P, 1], F32)
+            nc.scalar.mul(out=neg_mean_rstd[:], in_=neg_mean[:], mul=rstd[:])
+            z = norm.tile([P, D], F32)
+            nc.scalar.activation(
+                out=z[:], in_=y[:], func=ACT.Identity, bias=neg_mean_rstd[:], scale=rstd[:]
+            )
+            planes = norm.tile([P, PASSES, PACK, P], BF16)
+            for g in range(PASSES):
+                bank = psum_t.tile([P, PACK, P], F32, tag="tp")
+                for t in range(PACK):
+                    j = PACK * g + t
+                    nc.tensor.transpose(bank[:, t, :], z[:, P * j : P * (j + 1)], ident[:])
+                for t in range(PACK):
+                    j = PACK * g + t
+                    nc.scalar.activation(
+                        out=planes[:, g, t, :],
+                        in_=bank[:, t, :],
+                        func=ACT.Identity,
+                        bias=shift[:, j : j + 1],
+                        scale=gain[:, j : j + 1],
+                    )
+            local_grouped = norm.tile([P, D], BF16, align_bytes=64)
+            nc.vector.tensor_copy(
+                out=local_grouped[:].rearrange("q (g r t) -> q g r t", g=PASSES, t=PACK),
+                in_=planes[:].rearrange("q g t r -> q g r t"),
+            )
+            nc.vector.quantize_mx(
+                out=local_codes[:, i].rearrange("q g r -> q (g r)").bitcast(FP8X4),
+                scales=local_scales[:, i].rearrange("q g r -> q (g r)"),
+                in_=local_grouped[:],
+            )
+
+        for i in range(TOKEN_TILES):
+            for n in range(D3 // CHUNK):
+                cols = slice(CHUNK * n, CHUNK * (n + 1))
+                if n % STORE_CHUNKS == 0:
+                    result = out_pool.tile([P, STORE_CHUNKS * CHUNK], F32)
+                    first_col = CHUNK * n
+                acc = psum_acc.tile([P, CHUNK], F32, tag="acc")
+                for g in range(PASSES):
+                    nc.tensor.matmul_mx(
+                        out=acc[:],
+                        lhsT=local_codes[:, i, g, :].bitcast(FP8X4),
+                        lhsT_scale=local_scales[:, i, g, :],
+                        rhs=wqkv_codes[:, g, cols].bitcast(FP8X4),
+                        rhs_scale=wqkv_scales[:, g, cols],
+                        start=(g == 0),
+                        stop=(g == PASSES - 1),
+                    )
+                nc.vector.tensor_tensor(
+                    out=result[:, CHUNK * n - first_col : CHUNK * (n + 1) - first_col],
+                    in0=acc[:],
+                    in1=bqkv_rows[:, cols],
+                    op=ALU.add,
+                )
+                if n % STORE_CHUNKS == STORE_CHUNKS - 1:
+                    nc.sync.dma_start(out=out[:, i, first_col : CHUNK * (n + 1)], in_=result[:])

@@ -23,39 +23,13 @@ PAIRS = 2
 WORDS_PER_PASS = K_PASS // PAIRS
 CHUNK = 512
 ROW_TILES = CHUNK // P
-STORE_CHUNKS = 3
+FEATURE_TILES = D // P
+SWEEPS = 2
+SWEEP_CHUNKS = D3 // CHUNK // SWEEPS
+EARLY_UNITS = 2
+FIRST_ROUND = -5
 
 FLOPS = 2 * P * TOKEN_TILES * D * (D + D3)
-
-
-def copy_bank(nc, on_vector, out, in_):
-    if on_vector:
-        nc.vector.tensor_copy(out=out, in_=in_)
-    else:
-        nc.scalar.copy(out=out, in_=in_)
-
-
-def quantise_weight_chunk(nc, stage, psum_t, ident, row_tiles, codes, scales, share_with_vector):
-    for g in range(PASSES):
-        grouped = stage.tile([P, PACK * CHUNK], BF16, align_bytes=64, tag="w_grouped")
-        grouped_words = grouped[:].bitcast(F32).rearrange("q (n u) -> q n u", u=PAIRS)
-        for half in range(2):
-            bank = psum_t.tile([P, PAIRS, 2, P], F32, tag="tp")
-            for u in range(PAIRS):
-                first = WORDS_PER_PASS * g + P * u
-                for j in range(2):
-                    nc.tensor.transpose(
-                        bank[:, u, j, :], row_tiles[2 * half + j][:, first : first + P], ident[:]
-                    )
-            copy_bank(
-                nc,
-                share_with_vector and half == 1,
-                out=grouped_words[:, 2 * P * half : 2 * P * (half + 1), :],
-                in_=bank[:].rearrange("q u j r -> q (j r) u"),
-            )
-        nc.vector.quantize_mx(
-            out=codes[:, g, :].bitcast(FP8X4), scales=scales[:, g, :], in_=grouped[:]
-        )
 
 
 def tile_hlgan_pb_kernel(tc, attn_l, wo_l, bo_l, g1, be1, wqkv_g, bqkv_g, out):
@@ -63,20 +37,64 @@ def tile_hlgan_pb_kernel(tc, attn_l, wo_l, bo_l, g1, be1, wqkv_g, bqkv_g, out):
     with ExitStack() as ctx:
         const = ctx.enter_context(tc.tile_pool(name="const", bufs=1))
         keep = ctx.enter_context(tc.tile_pool(name="keep", bufs=1))
-        raw = ctx.enter_context(tc.tile_pool(name="raw", bufs=1))
         stage = ctx.enter_context(tc.tile_pool(name="stage", bufs=2))
         norm = ctx.enter_context(tc.tile_pool(name="norm", bufs=2))
-        small = ctx.enter_context(tc.tile_pool(name="small", bufs=4))
-        out_pool = ctx.enter_context(tc.tile_pool(name="out_pool", bufs=4))
-        psum_t = ctx.enter_context(tc.psum_pool(name="psum_t", bufs=3))
-        psum_acc = ctx.enter_context(tc.psum_pool(name="psum_acc", bufs=5))
+        small = ctx.enter_context(tc.tile_pool(name="small", bufs=3))
+        out_pool = ctx.enter_context(tc.tile_pool(name="out_pool", bufs=3))
+        psum_t = ctx.enter_context(tc.psum_pool(name="psum_t", bufs=4))
+        psum_acc = ctx.enter_context(tc.psum_pool(name="psum_acc", bufs=4))
+        ctx.enter_context(tc.manual_schedule())
 
         ident = const.tile([P, P], F32)
         make_identity(nc, ident[:])
         eps = const.tile([P, 1], F32)
         nc.vector.memset(eps[:], EPS)
         warm = const.tile([P, 1], F32)
-        nc.scalar.activation(out=warm[:], in_=eps[:], func=ACT.Sqrt)
+        nc.scalar.activation(out=warm[:], in_=eps[:], func=ACT.Abs_reciprocal_sqrt)
+
+        bo_rows = const.tile([P, D], BF16)
+        nc.scalar.dma_start(out=bo_rows[:], in_=bo_l.partition_broadcast(P))
+        g_raw = const.tile([P, FEATURE_TILES], BF16)
+        nc.scalar.dma_start(
+            out=g_raw[:].rearrange("q (a e) -> q a e", e=PAIRS),
+            in_=g1.rearrange("(a q e) -> q a e", q=P, e=PAIRS),
+        )
+        be_raw = const.tile([P, FEATURE_TILES], BF16)
+        nc.scalar.dma_start(
+            out=be_raw[:].rearrange("q (a e) -> q a e", e=PAIRS),
+            in_=be1.rearrange("(a q e) -> q a e", q=P, e=PAIRS),
+        )
+
+        wo_raw = keep.tile([P, FEATURE_TILES // PAIRS, PAIRS, D], BF16)
+        wo_view = wo_l.rearrange("(a q e) k -> q a e k", q=P, e=PAIRS)
+        for a in range(0, FEATURE_TILES // PAIRS, 2):
+            nc.sync.dma_start(out=wo_raw[:, a : a + 2], in_=wo_view[:, a : a + 2])
+        x_raw = keep.tile([P, TOKEN_TILES, D], BF16)
+        wqkv_raw = keep.tile([P, D3 // P, D], BF16)
+        bqkv_rows = const.tile([P, D3], BF16)
+        for n in range(D3 // CHUNK):
+            if 2 * n < TOKEN_TILES:
+                nc.sync.dma_start(out=x_raw[:, 2 * n : 2 * n + 2, :], in_=attn_l[:, 2 * n : 2 * n + 2, :])
+            nc.sync.dma_start(
+                out=wqkv_raw[:, ROW_TILES * n : ROW_TILES * (n + 1), :],
+                in_=wqkv_g[CHUNK * n : CHUNK * (n + 1), :].rearrange("(j p) k -> p j k", p=P),
+            )
+            if n == SWEEP_CHUNKS - 1:
+                nc.sync.dma_start(out=bqkv_rows[:], in_=bqkv_g.partition_broadcast(P))
+
+        bo_cols = const.tile([P, D], BF16)
+        nc.gpsimd.tensor_scalar(
+            out=bo_cols[:].rearrange("p (a e q) -> p a e q", e=PAIRS, q=P),
+            in0=bo_rows[:].rearrange("p (a q e) -> p a e q", q=P, e=PAIRS),
+            scalar1=1.0,
+            scalar2=0.0,
+            op0=ALU.mult,
+            op1=ALU.add,
+        )
+        gain = const.tile([P, FEATURE_TILES], F32)
+        nc.gpsimd.tensor_copy(out=gain[:], in_=g_raw[:])
+        shift = const.tile([P, FEATURE_TILES], F32)
+        nc.gpsimd.tensor_copy(out=shift[:], in_=be_raw[:])
 
         x_codes = keep.tile([P, TOKEN_TILES, PASSES, P], U32, align_bytes=64)
         x_scales = keep.tile([P, TOKEN_TILES, PASSES, P], U8, align_bytes=64)
@@ -86,187 +104,213 @@ def tile_hlgan_pb_kernel(tc, attn_l, wo_l, bo_l, g1, be1, wqkv_g, bqkv_g, out):
         local_scales = keep.tile([P, TOKEN_TILES, PASSES, P], U8, align_bytes=64)
         wqkv_codes = keep.tile([P, PASSES, D3], U32, align_bytes=64)
         wqkv_scales = keep.tile([P, PASSES, D3], U8, align_bytes=64)
-        wqkv_raw = keep.tile([P, D3 // P, D], BF16)
 
-        bo_rows = const.tile([P, D], BF16)
-        nc.scalar.dma_start(out=bo_rows[:], in_=bo_l.partition_broadcast(P))
-        g_raw = const.tile([P, D // P], BF16)
-        nc.scalar.dma_start(
-            out=g_raw[:].rearrange("q (a e) -> q a e", e=PAIRS),
-            in_=g1.rearrange("(a q e) -> q a e", q=P, e=PAIRS),
-        )
-        be_raw = const.tile([P, D // P], BF16)
-        nc.scalar.dma_start(
-            out=be_raw[:].rearrange("q (a e) -> q a e", e=PAIRS),
-            in_=be1.rearrange("(a q e) -> q a e", q=P, e=PAIRS),
-        )
-        bo_cols = const.tile([P, D], BF16)
-        nc.vector.tensor_copy(
-            out=bo_cols[:].rearrange("p (a e q) -> p a e q", e=PAIRS, q=P),
-            in_=bo_rows[:].rearrange("p (a q e) -> p a e q", q=P, e=PAIRS),
-        )
-        gain = const.tile([P, D // P], F32)
-        nc.vector.tensor_copy(out=gain[:], in_=g_raw[:])
-        shift = const.tile([P, D // P], F32)
-        nc.vector.tensor_copy(out=shift[:], in_=be_raw[:])
-
-        wo_raw = raw.tile([P, D // (PAIRS * P), PAIRS, D], BF16)
-        wo_view = wo_l.rearrange("(a q e) k -> q a e k", q=P, e=PAIRS)
-        for a in range(0, D // (PAIRS * P), 2):
-            nc.sync.dma_start(out=wo_raw[:, a : a + 2], in_=wo_view[:, a : a + 2])
-        x_raw = raw.tile([P, TOKEN_TILES, D], BF16)
-        for i in range(0, TOKEN_TILES, 2):
-            nc.sync.dma_start(out=x_raw[:, i : i + 2, :], in_=attn_l[:, i : i + 2, :])
-        for n in range(D3 // CHUNK):
-            nc.sync.dma_start(
-                out=wqkv_raw[:, ROW_TILES * n : ROW_TILES * (n + 1), :],
-                in_=wqkv_g[CHUNK * n : CHUNK * (n + 1), :].rearrange("(j p) k -> p j k", p=P),
-            )
-        bqkv_rows = const.tile([P, D3], BF16)
-        nc.sync.dma_start(out=bqkv_rows[:], in_=bqkv_g.partition_broadcast(P))
-
+        units = []
         for h in range(D // CHUNK):
             cols = slice(CHUNK * h, CHUNK * (h + 1))
-            quantise_weight_chunk(
-                nc,
-                stage,
-                psum_t,
-                ident,
-                [wo_raw[:, 2 * h + j // 2, j % 2, :].bitcast(F32) for j in range(ROW_TILES)],
-                wo_codes[:, :, cols],
-                wo_scales[:, :, cols],
-                True,
-            )
-        for i in range(TOKEN_TILES):
+            rows = [wo_raw[:, 2 * h + j // 2, j % 2, :].bitcast(F32) for j in range(ROW_TILES)]
+            for g in range(PASSES):
+                units.append((rows, g, wo_codes[:, g, cols], wo_scales[:, g, cols]))
+        for n in range(D3 // CHUNK):
+            cols = slice(CHUNK * n, CHUNK * (n + 1))
+            rows = [wqkv_raw[:, ROW_TILES * n + j, :].bitcast(F32) for j in range(ROW_TILES)]
+            for g in range(PASSES):
+                units.append((rows, g, wqkv_codes[:, g, cols], wqkv_scales[:, g, cols]))
+
+        def units_of_round(r):
+            if r < 0:
+                first = EARLY_UNITS * (r - FIRST_ROUND)
+                return range(first, first + EARLY_UNITS)
+            first = EARLY_UNITS * (-FIRST_ROUND) + r
+            return range(first, min(first + 1, len(units)))
+
+        def live(i):
+            return 0 <= i < TOKEN_TILES
+
+        w_grouped, x_grouped, y, y_sum, neg_mean, sum_sq = {}, {}, {}, {}, {}, {}
+        rstd, neg_mean_rstd, z, planes = {}, {}, {}, {}
+
+        def transpose_weight_half(k, half, on_vector):
+            rows, g = units[k][0], units[k][1]
+            if half == 0:
+                grouped = stage.tile([P, PACK * CHUNK], BF16, align_bytes=64, tag="w_grouped", bufs=4)
+                w_grouped[k] = grouped
+            bank = psum_t.tile([P, PAIRS, 2, P], F32, tag="tp")
+            for u in range(PAIRS):
+                first = WORDS_PER_PASS * g + P * u
+                for j in range(2):
+                    nc.tensor.transpose(bank[:, u, j, :], rows[2 * half + j][:, first : first + P], ident[:])
+            words = w_grouped[k][:].bitcast(F32).rearrange("q (n u) -> q n u", u=PAIRS)
+            dst = words[:, 2 * P * half : 2 * P * (half + 1), :]
+            src = bank[:].rearrange("q u j r -> q (j r) u")
+            if on_vector:
+                nc.vector.tensor_copy(out=dst, in_=src)
+            else:
+                nc.scalar.copy(out=dst, in_=src)
+
+        def transpose_tokens(i):
             x_words = x_raw[:, i, :].bitcast(F32)
             bank = psum_t.tile([P, PASSES, PAIRS, P], F32, tag="tp")
             for g in range(PASSES):
                 for u in range(PAIRS):
                     first = WORDS_PER_PASS * g + P * u
                     nc.tensor.transpose(bank[:, g, u, :], x_words[:, first : first + P], ident[:])
-            x_grouped = stage.tile([P, D], BF16, align_bytes=64)
-            copy_bank(
-                nc,
-                i % 2 == 1,
-                out=x_grouped[:].bitcast(F32).rearrange("q (g r u) -> q g r u", g=PASSES, u=PAIRS),
+            grouped = stage.tile([P, D], BF16, align_bytes=64, tag="x_grouped")
+            nc.vector.tensor_copy(
+                out=grouped[:].bitcast(F32).rearrange("q (g r u) -> q g r u", g=PASSES, u=PAIRS),
                 in_=bank[:].rearrange("q g u r -> q g r u"),
             )
+            x_grouped[i] = grouped
+
+        def quantise_tile(grouped, codes, scales, i):
             nc.vector.quantize_mx(
-                out=x_codes[:, i].rearrange("q g r -> q (g r)").bitcast(FP8X4),
-                scales=x_scales[:, i].rearrange("q g r -> q (g r)"),
-                in_=x_grouped[:],
+                out=codes[:, i].rearrange("q g r -> q (g r)").bitcast(FP8X4),
+                scales=scales[:, i].rearrange("q g r -> q (g r)"),
+                in_=grouped[:],
             )
 
-        for n in range(D3 // CHUNK):
-            cols = slice(CHUNK * n, CHUNK * (n + 1))
-            quantise_weight_chunk(
-                nc,
-                stage,
-                psum_t,
-                ident,
-                [wqkv_raw[:, ROW_TILES * n + j, :].bitcast(F32) for j in range(ROW_TILES)],
-                wqkv_codes[:, :, cols],
-                wqkv_scales[:, :, cols],
-                False,
-            )
+        def multiply(acc, a_codes, a_scales, i, b_codes, b_scales, cols):
+            for g in range(PASSES):
+                nc.tensor.matmul_mx(
+                    out=acc[:],
+                    lhsT=a_codes[:, i, g, :].bitcast(FP8X4),
+                    lhsT_scale=a_scales[:, i, g, :],
+                    rhs=b_codes[:, g, cols].bitcast(FP8X4),
+                    rhs_scale=b_scales[:, g, cols],
+                    start=(g == 0),
+                    stop=(g == PASSES - 1),
+                )
 
-        for i in range(TOKEN_TILES):
-            y = norm.tile([P, D], F32, bufs=3)
-            y_sum = small.tile([P, D // CHUNK], F32)
+        def project(i):
+            y_tile = norm.tile([P, D], F32, tag="y")
+            sums = small.tile([P, D // CHUNK], F32, tag="y_sum")
             for h in range(D // CHUNK):
                 cols = slice(CHUNK * h, CHUNK * (h + 1))
                 acc = psum_acc.tile([P, CHUNK], F32, tag="acc")
-                for g in range(PASSES):
-                    nc.tensor.matmul_mx(
-                        out=acc[:],
-                        lhsT=x_codes[:, i, g, :].bitcast(FP8X4),
-                        lhsT_scale=x_scales[:, i, g, :],
-                        rhs=wo_codes[:, g, cols].bitcast(FP8X4),
-                        rhs_scale=wo_scales[:, g, cols],
-                        start=(g == 0),
-                        stop=(g == PASSES - 1),
-                    )
+                multiply(acc, x_codes, x_scales, i, wo_codes, wo_scales, cols)
                 nc.vector.scalar_tensor_tensor(
-                    out=y[:, cols],
+                    out=y_tile[:, cols],
                     in0=acc[:],
                     scalar=0.0,
                     in1=bo_cols[:, cols],
                     op0=ALU.add,
                     op1=ALU.add,
-                    accum_out=y_sum[:, h : h + 1],
+                    accum_out=sums[:, h : h + 1],
                 )
-            neg_mean = small.tile([P, 1], F32)
-            nc.vector.tensor_scalar(
-                out=neg_mean[:],
-                in0=y_sum[:, 0:1],
-                scalar1=y_sum[:, 1:2],
-                scalar2=-1.0 / D,
-                op0=ALU.add,
-                op1=ALU.mult,
-            )
-            squares = norm.tile([P, D], BF16)
-            sum_sq = small.tile([P, 1], F32)
+            y[i] = y_tile
+            y_sum[i] = sums
+
+        def mean_step(i):
+            scaled = small.tile([P, D // CHUNK], F32, tag="scaled")
+            result = small.tile([P, 1], F32, tag="neg_mean")
             nc.scalar.activation(
-                out=squares[:], in_=y[:], func=ACT.Square, bias=neg_mean[:], accum_out=sum_sq[:]
+                out=scaled[:], in_=y_sum[i][:], func=ACT.Copy, scale=-1.0 / D, accum_out=result[:]
             )
-            std = small.tile([P, 1], F32)
-            nc.scalar.activation(out=std[:], in_=sum_sq[:], func=ACT.Sqrt, bias=eps[:], scale=1.0 / D)
-            rstd = small.tile([P, 1], F32)
-            nc.vector.reciprocal(out=rstd[:], in_=std[:])
-            neg_mean_rstd = small.tile([P, 1], F32)
-            nc.scalar.mul(out=neg_mean_rstd[:], in_=neg_mean[:], mul=rstd[:])
-            z = norm.tile([P, D], F32)
+            neg_mean[i] = result
+
+        def squares_step(i):
+            squares = norm.tile([P, D], BF16, tag="squares")
+            result = small.tile([P, 1], F32, tag="sum_sq")
             nc.scalar.activation(
-                out=z[:], in_=y[:], func=ACT.Identity, bias=neg_mean_rstd[:], scale=rstd[:]
+                out=squares[:], in_=y[i][:], func=ACT.Square, bias=neg_mean[i][:], accum_out=result[:]
             )
-            planes = norm.tile([P, PASSES, PACK, P], BF16)
-            for g in range(PASSES):
-                bank = psum_t.tile([P, PACK, P], F32, tag="tp")
-                for t in range(PACK):
-                    j = PACK * g + t
-                    nc.tensor.transpose(bank[:, t, :], z[:, P * j : P * (j + 1)], ident[:])
-                for t in range(PACK):
-                    j = PACK * g + t
-                    nc.scalar.activation(
-                        out=planes[:, g, t, :],
-                        in_=bank[:, t, :],
-                        func=ACT.Identity,
-                        bias=shift[:, j : j + 1],
-                        scale=gain[:, j : j + 1],
-                    )
-            local_grouped = norm.tile([P, D], BF16, align_bytes=64)
+            sum_sq[i] = result
+
+        def rstd_step(i):
+            result = small.tile([P, 1], F32, tag="rstd")
+            nc.scalar.activation(
+                out=result[:], in_=sum_sq[i][:], func=ACT.Abs_reciprocal_sqrt, bias=eps[:], scale=1.0 / D
+            )
+            rstd[i] = result
+
+        def offset_step(i):
+            result = small.tile([P, 1], F32, tag="neg_mean_rstd")
+            nc.scalar.mul(out=result[:], in_=neg_mean[i][:], mul=rstd[i][:])
+            neg_mean_rstd[i] = result
+
+        def normalise_step(i):
+            result = norm.tile([P, D], F32, tag="z")
+            nc.scalar.activation(
+                out=result[:], in_=y[i][:], func=ACT.Identity, bias=neg_mean_rstd[i][:], scale=rstd[i][:]
+            )
+            z[i] = result
+
+        def turn_pass(i, g):
+            if g == 0:
+                tile_planes = norm.tile([P, PASSES, PACK, P], BF16, tag="planes")
+                planes[i] = tile_planes
+            bank = psum_t.tile([P, PACK, P], F32, tag="tp")
+            for t in range(PACK):
+                j = PACK * g + t
+                nc.tensor.transpose(bank[:, t, :], z[i][:, P * j : P * (j + 1)], ident[:])
+            for t in range(PACK):
+                j = PACK * g + t
+                nc.scalar.activation(
+                    out=planes[i][:, g, t, :],
+                    in_=bank[:, t, :],
+                    func=ACT.Identity,
+                    bias=shift[:, j : j + 1],
+                    scale=gain[:, j : j + 1],
+                )
+
+        def group_local(i):
+            grouped = norm.tile([P, D], BF16, align_bytes=64, tag="local_grouped")
             nc.vector.tensor_copy(
-                out=local_grouped[:].rearrange("q (g r t) -> q g r t", g=PASSES, t=PACK),
-                in_=planes[:].rearrange("q g t r -> q g r t"),
+                out=grouped[:].rearrange("q (g r t) -> q g r t", g=PASSES, t=PACK),
+                in_=planes[i][:].rearrange("q g t r -> q g r t"),
             )
-            nc.vector.quantize_mx(
-                out=local_codes[:, i].rearrange("q g r -> q (g r)").bitcast(FP8X4),
-                scales=local_scales[:, i].rearrange("q g r -> q (g r)"),
-                in_=local_grouped[:],
-            )
+            return grouped
+
+        def qkv(i, sweep):
+            result = out_pool.tile([P, SWEEP_CHUNKS * CHUNK], F32, tag="result")
+            first_col = SWEEP_CHUNKS * CHUNK * sweep
+            for n in range(SWEEP_CHUNKS):
+                cols = slice(first_col + CHUNK * n, first_col + CHUNK * (n + 1))
+                acc = psum_acc.tile([P, CHUNK], F32, tag="acc")
+                multiply(acc, local_codes, local_scales, i, wqkv_codes, wqkv_scales, cols)
+                nc.vector.tensor_tensor(
+                    out=result[:, CHUNK * n : CHUNK * (n + 1)], in0=acc[:], in1=bqkv_rows[:, cols], op=ALU.add
+                )
+            nc.sync.dma_start(out=out[:, i, first_col : first_col + SWEEP_CHUNKS * CHUNK], in_=result[:])
+
+        copied = []
+        for r in range(FIRST_ROUND, TOKEN_TILES):
+            for k in copied:
+                nc.vector.quantize_mx(
+                    out=units[k][2].bitcast(FP8X4), scales=units[k][3], in_=w_grouped[k][:]
+                )
+            copied = list(units_of_round(r))
+            banks = [(k, half) for k in copied for half in range(2)]
+            if live(r + 2):
+                mean_step(r + 2)
+            for k, half in banks[: len(banks) // 2]:
+                transpose_weight_half(k, half, r < 0 and half == 1)
+            if live(r + 2):
+                squares_step(r + 2)
+            for k, half in banks[len(banks) // 2 :]:
+                transpose_weight_half(k, half, r < 0 and half == 1)
+            if live(r + 4):
+                transpose_tokens(r + 4)
+            if live(r + 2):
+                rstd_step(r + 2)
+            if live(r + 1):
+                turn_pass(r + 1, 0)
+            if live(r + 2):
+                offset_step(r + 2)
+            if live(r + 1):
+                turn_pass(r + 1, 1)
+            if live(r + 2):
+                normalise_step(r + 2)
+            if live(r):
+                qkv(r, 0)
+            if live(r + 1):
+                local_grouped = group_local(r + 1)
+            if live(r + 4):
+                quantise_tile(x_grouped[r + 4], x_codes, x_scales, r + 4)
+            if live(r + 1):
+                quantise_tile(local_grouped, local_codes, local_scales, r + 1)
+            if live(r + 3):
+                project(r + 3)
 
         for i in range(TOKEN_TILES):
-            for n in range(D3 // CHUNK):
-                cols = slice(CHUNK * n, CHUNK * (n + 1))
-                if n % STORE_CHUNKS == 0:
-                    result = out_pool.tile([P, STORE_CHUNKS * CHUNK], F32)
-                    first_col = CHUNK * n
-                acc = psum_acc.tile([P, CHUNK], F32, tag="acc")
-                for g in range(PASSES):
-                    nc.tensor.matmul_mx(
-                        out=acc[:],
-                        lhsT=local_codes[:, i, g, :].bitcast(FP8X4),
-                        lhsT_scale=local_scales[:, i, g, :],
-                        rhs=wqkv_codes[:, g, cols].bitcast(FP8X4),
-                        rhs_scale=wqkv_scales[:, g, cols],
-                        start=(g == 0),
-                        stop=(g == PASSES - 1),
-                    )
-                nc.vector.tensor_tensor(
-                    out=result[:, CHUNK * n - first_col : CHUNK * (n + 1) - first_col],
-                    in0=acc[:],
-                    in1=bqkv_rows[:, cols],
-                    op=ALU.add,
-                )
-                if n % STORE_CHUNKS == STORE_CHUNKS - 1:
-                    nc.sync.dma_start(out=out[:, i, first_col : CHUNK * (n + 1)], in_=result[:])
+            qkv(i, 1)

@@ -24,10 +24,13 @@ WORDS_PER_PASS = K_PASS // PAIRS
 CHUNK = 512
 ROW_TILES = CHUNK // P
 FEATURE_TILES = D // P
-SWEEPS = 2
-SWEEP_CHUNKS = D3 // CHUNK // SWEEPS
-EARLY_UNITS = 2
-FIRST_ROUND = -5
+
+TOKENS_AHEAD = 7
+PROJECT_AHEAD = 6
+NORM_AHEAD = 3
+TURN_AHEAD = 2
+UNITS_A_ROUND = 2
+FIRST_ROUND = -((D + D3) // CHUNK * PASSES // UNITS_A_ROUND)
 
 FLOPS = 2 * P * TOKEN_TILES * D * (D + D3)
 
@@ -39,10 +42,10 @@ def tile_hlgan_pb_kernel(tc, attn_l, wo_l, bo_l, g1, be1, wqkv_g, bqkv_g, out):
         keep = ctx.enter_context(tc.tile_pool(name="keep", bufs=1))
         stage = ctx.enter_context(tc.tile_pool(name="stage", bufs=2))
         norm = ctx.enter_context(tc.tile_pool(name="norm", bufs=2))
-        small = ctx.enter_context(tc.tile_pool(name="small", bufs=3))
-        out_pool = ctx.enter_context(tc.tile_pool(name="out_pool", bufs=3))
-        psum_t = ctx.enter_context(tc.psum_pool(name="psum_t", bufs=4))
-        psum_acc = ctx.enter_context(tc.psum_pool(name="psum_acc", bufs=4))
+        small = ctx.enter_context(tc.tile_pool(name="small", bufs=2))
+        out_pool = ctx.enter_context(tc.tile_pool(name="out_pool", bufs=8))
+        psum_t = ctx.enter_context(tc.psum_pool(name="psum_t", bufs=5))
+        psum_acc = ctx.enter_context(tc.psum_pool(name="psum_acc", bufs=3))
         ctx.enter_context(tc.manual_schedule())
 
         ident = const.tile([P, P], F32)
@@ -70,17 +73,18 @@ def tile_hlgan_pb_kernel(tc, attn_l, wo_l, bo_l, g1, be1, wqkv_g, bqkv_g, out):
         for a in range(0, FEATURE_TILES // PAIRS, 2):
             nc.sync.dma_start(out=wo_raw[:, a : a + 2], in_=wo_view[:, a : a + 2])
         x_raw = keep.tile([P, TOKEN_TILES, D], BF16)
-        wqkv_raw = keep.tile([P, D3 // P, D], BF16)
-        bqkv_rows = const.tile([P, D3], BF16)
+        wqkv_raw = []
         for n in range(D3 // CHUNK):
             if 2 * n < TOKEN_TILES:
                 nc.sync.dma_start(out=x_raw[:, 2 * n : 2 * n + 2, :], in_=attn_l[:, 2 * n : 2 * n + 2, :])
+            chunk_rows = stage.tile([P, ROW_TILES, D], BF16, tag="wqkv_raw", bufs=4)
             nc.sync.dma_start(
-                out=wqkv_raw[:, ROW_TILES * n : ROW_TILES * (n + 1), :],
+                out=chunk_rows[:],
                 in_=wqkv_g[CHUNK * n : CHUNK * (n + 1), :].rearrange("(j p) k -> p j k", p=P),
             )
-            if n == SWEEP_CHUNKS - 1:
-                nc.sync.dma_start(out=bqkv_rows[:], in_=bqkv_g.partition_broadcast(P))
+            wqkv_raw.append(chunk_rows)
+        bqkv_rows = const.tile([P, D3], BF16)
+        nc.sync.dma_start(out=bqkv_rows[:], in_=bqkv_g.partition_broadcast(P))
 
         bo_cols = const.tile([P, D], BF16)
         nc.gpsimd.tensor_scalar(
@@ -113,16 +117,9 @@ def tile_hlgan_pb_kernel(tc, attn_l, wo_l, bo_l, g1, be1, wqkv_g, bqkv_g, out):
                 units.append((rows, g, wo_codes[:, g, cols], wo_scales[:, g, cols]))
         for n in range(D3 // CHUNK):
             cols = slice(CHUNK * n, CHUNK * (n + 1))
-            rows = [wqkv_raw[:, ROW_TILES * n + j, :].bitcast(F32) for j in range(ROW_TILES)]
+            rows = [wqkv_raw[n][:, j, :].bitcast(F32) for j in range(ROW_TILES)]
             for g in range(PASSES):
                 units.append((rows, g, wqkv_codes[:, g, cols], wqkv_scales[:, g, cols]))
-
-        def units_of_round(r):
-            if r < 0:
-                first = EARLY_UNITS * (r - FIRST_ROUND)
-                return range(first, first + EARLY_UNITS)
-            first = EARLY_UNITS * (-FIRST_ROUND) + r
-            return range(first, min(first + 1, len(units)))
 
         def live(i):
             return 0 <= i < TOKEN_TILES
@@ -130,17 +127,17 @@ def tile_hlgan_pb_kernel(tc, attn_l, wo_l, bo_l, g1, be1, wqkv_g, bqkv_g, out):
         w_grouped, x_grouped, y, y_sum, neg_mean, sum_sq = {}, {}, {}, {}, {}, {}
         rstd, neg_mean_rstd, z, planes = {}, {}, {}, {}
 
-        def transpose_weight_half(k, half, on_vector):
-            rows, g = units[k][0], units[k][1]
+        def transpose_weight_half(w, half, on_vector):
+            rows, g = units[w][0], units[w][1]
             if half == 0:
                 grouped = stage.tile([P, PACK * CHUNK], BF16, align_bytes=64, tag="w_grouped", bufs=4)
-                w_grouped[k] = grouped
+                w_grouped[w] = grouped
             bank = psum_t.tile([P, PAIRS, 2, P], F32, tag="tp")
             for u in range(PAIRS):
                 first = WORDS_PER_PASS * g + P * u
                 for j in range(2):
                     nc.tensor.transpose(bank[:, u, j, :], rows[2 * half + j][:, first : first + P], ident[:])
-            words = w_grouped[k][:].bitcast(F32).rearrange("q (n u) -> q n u", u=PAIRS)
+            words = w_grouped[w][:].bitcast(F32).rearrange("q (n u) -> q n u", u=PAIRS)
             dst = words[:, 2 * P * half : 2 * P * (half + 1), :]
             src = bank[:].rearrange("q u j r -> q (j r) u")
             if on_vector:
@@ -156,7 +153,7 @@ def tile_hlgan_pb_kernel(tc, attn_l, wo_l, bo_l, g1, be1, wqkv_g, bqkv_g, out):
                     first = WORDS_PER_PASS * g + P * u
                     nc.tensor.transpose(bank[:, g, u, :], x_words[:, first : first + P], ident[:])
             grouped = stage.tile([P, D], BF16, align_bytes=64, tag="x_grouped")
-            nc.vector.tensor_copy(
+            nc.scalar.copy(
                 out=grouped[:].bitcast(F32).rearrange("q (g r u) -> q g r u", g=PASSES, u=PAIRS),
                 in_=bank[:].rearrange("q g u r -> q g r u"),
             )
@@ -182,8 +179,9 @@ def tile_hlgan_pb_kernel(tc, attn_l, wo_l, bo_l, g1, be1, wqkv_g, bqkv_g, out):
                 )
 
         def project(i):
-            y_tile = norm.tile([P, D], F32, tag="y")
-            sums = small.tile([P, D // CHUNK], F32, tag="y_sum")
+            in_flight = PROJECT_AHEAD - NORM_AHEAD + 2
+            y_tile = norm.tile([P, D], F32, tag="y", bufs=in_flight)
+            sums = small.tile([P, D // CHUNK], F32, tag="y_sum", bufs=in_flight)
             for h in range(D // CHUNK):
                 cols = slice(CHUNK * h, CHUNK * (h + 1))
                 acc = psum_acc.tile([P, CHUNK], F32, tag="acc")
@@ -209,7 +207,7 @@ def tile_hlgan_pb_kernel(tc, attn_l, wo_l, bo_l, g1, be1, wqkv_g, bqkv_g, out):
             neg_mean[i] = result
 
         def squares_step(i):
-            squares = norm.tile([P, D], BF16, tag="squares")
+            squares = norm.tile([P, D], BF16, tag="squares", bufs=1)
             result = small.tile([P, 1], F32, tag="sum_sq")
             nc.scalar.activation(
                 out=squares[:], in_=y[i][:], func=ACT.Square, bias=neg_mean[i][:], accum_out=result[:]
@@ -229,7 +227,7 @@ def tile_hlgan_pb_kernel(tc, attn_l, wo_l, bo_l, g1, be1, wqkv_g, bqkv_g, out):
             neg_mean_rstd[i] = result
 
         def normalise_step(i):
-            result = norm.tile([P, D], F32, tag="z")
+            result = norm.tile([P, D], F32, tag="z", bufs=3)
             nc.scalar.activation(
                 out=result[:], in_=y[i][:], func=ACT.Identity, bias=neg_mean_rstd[i][:], scale=rstd[i][:]
             )
@@ -256,61 +254,59 @@ def tile_hlgan_pb_kernel(tc, attn_l, wo_l, bo_l, g1, be1, wqkv_g, bqkv_g, out):
         def group_local(i):
             grouped = norm.tile([P, D], BF16, align_bytes=64, tag="local_grouped")
             nc.vector.tensor_copy(
-                out=grouped[:].rearrange("q (g r t) -> q g r t", g=PASSES, t=PACK),
-                in_=planes[i][:].rearrange("q g t r -> q g r t"),
+                out=grouped[:].rearrange("q (g c i t) -> q g c t i", g=PASSES, i=4, t=PACK),
+                in_=planes[i][:].rearrange("q g t (c i) -> q g c t i", i=4),
             )
             return grouped
 
-        def qkv(i, sweep):
-            result = out_pool.tile([P, SWEEP_CHUNKS * CHUNK], F32, tag="result")
-            first_col = SWEEP_CHUNKS * CHUNK * sweep
-            for n in range(SWEEP_CHUNKS):
-                cols = slice(first_col + CHUNK * n, first_col + CHUNK * (n + 1))
+        def qkv(i):
+            for n in range(D3 // CHUNK):
+                cols = slice(CHUNK * n, CHUNK * (n + 1))
                 acc = psum_acc.tile([P, CHUNK], F32, tag="acc")
                 multiply(acc, local_codes, local_scales, i, wqkv_codes, wqkv_scales, cols)
-                nc.vector.tensor_tensor(
-                    out=result[:, CHUNK * n : CHUNK * (n + 1)], in0=acc[:], in1=bqkv_rows[:, cols], op=ALU.add
-                )
-            nc.sync.dma_start(out=out[:, i, first_col : first_col + SWEEP_CHUNKS * CHUNK], in_=result[:])
+                result = out_pool.tile([P, CHUNK], F32, tag="result")
+                nc.vector.tensor_tensor(out=result[:], in0=acc[:], in1=bqkv_rows[:, cols], op=ALU.add)
+                nc.sync.dma_start(out=out[:, i, cols], in_=result[:])
 
         copied = []
         for r in range(FIRST_ROUND, TOKEN_TILES):
-            for k in copied:
+            for w in copied:
                 nc.vector.quantize_mx(
-                    out=units[k][2].bitcast(FP8X4), scales=units[k][3], in_=w_grouped[k][:]
+                    out=units[w][2].bitcast(FP8X4), scales=units[w][3], in_=w_grouped[w][:]
                 )
-            copied = list(units_of_round(r))
-            banks = [(k, half) for k in copied for half in range(2)]
-            if live(r + 2):
-                mean_step(r + 2)
-            for k, half in banks[: len(banks) // 2]:
-                transpose_weight_half(k, half, r < 0 and half == 1)
-            if live(r + 2):
-                squares_step(r + 2)
-            for k, half in banks[len(banks) // 2 :]:
-                transpose_weight_half(k, half, r < 0 and half == 1)
-            if live(r + 4):
-                transpose_tokens(r + 4)
-            if live(r + 2):
-                rstd_step(r + 2)
-            if live(r + 1):
-                turn_pass(r + 1, 0)
-            if live(r + 2):
-                offset_step(r + 2)
-            if live(r + 1):
-                turn_pass(r + 1, 1)
-            if live(r + 2):
-                normalise_step(r + 2)
+            copied = []
+            if r < 0:
+                first_unit = UNITS_A_ROUND * (r - FIRST_ROUND)
+                copied = list(range(first_unit, first_unit + UNITS_A_ROUND))
+            for w in copied[:1]:
+                transpose_weight_half(w, 0, False)
+                transpose_weight_half(w, 1, live(r + NORM_AHEAD))
+            if live(r + NORM_AHEAD):
+                mean_step(r + NORM_AHEAD)
+            for w in copied[1:]:
+                transpose_weight_half(w, 0, False)
+                transpose_weight_half(w, 1, live(r + NORM_AHEAD))
+            if live(r + NORM_AHEAD):
+                squares_step(r + NORM_AHEAD)
+            if live(r + TOKENS_AHEAD):
+                transpose_tokens(r + TOKENS_AHEAD)
+            if live(r + NORM_AHEAD):
+                rstd_step(r + NORM_AHEAD)
+            if live(r + TURN_AHEAD):
+                turn_pass(r + TURN_AHEAD, 0)
+            if live(r + NORM_AHEAD):
+                offset_step(r + NORM_AHEAD)
+            if live(r + TURN_AHEAD):
+                turn_pass(r + TURN_AHEAD, 1)
+            if live(r + NORM_AHEAD):
+                normalise_step(r + NORM_AHEAD)
             if live(r):
-                qkv(r, 0)
-            if live(r + 1):
-                local_grouped = group_local(r + 1)
-            if live(r + 4):
-                quantise_tile(x_grouped[r + 4], x_codes, x_scales, r + 4)
-            if live(r + 1):
-                quantise_tile(local_grouped, local_codes, local_scales, r + 1)
-            if live(r + 3):
-                project(r + 3)
-
-        for i in range(TOKEN_TILES):
-            qkv(i, 1)
+                qkv(r)
+            if live(r + PROJECT_AHEAD):
+                project(r + PROJECT_AHEAD)
+            if live(r + TURN_AHEAD):
+                local_grouped = group_local(r + TURN_AHEAD)
+            if live(r + TOKENS_AHEAD):
+                quantise_tile(x_grouped[r + TOKENS_AHEAD], x_codes, x_scales, r + TOKENS_AHEAD)
+            if live(r + TURN_AHEAD):
+                quantise_tile(local_grouped, local_codes, local_scales, r + TURN_AHEAD)

@@ -48,6 +48,8 @@ def tile_hlgan_pb_kernel(tc, attn_l, wo_l, bo_l, g1, be1, wqkv_g, bqkv_g, out):
         psum_acc = ctx.enter_context(tc.psum_pool(name="psum_acc", bufs=3))
         ctx.enter_context(tc.manual_schedule())
 
+        bo_row = const.tile([P, D], BF16)
+        nc.vector.memset(bo_row[:], 0.0)
         ident = const.tile([P, P], F32)
         make_identity(nc, ident[:])
         eps = const.tile([P, 1], F32)
@@ -55,26 +57,15 @@ def tile_hlgan_pb_kernel(tc, attn_l, wo_l, bo_l, g1, be1, wqkv_g, bqkv_g, out):
         warm = const.tile([P, 1], F32)
         nc.scalar.activation(out=warm[:], in_=eps[:], func=ACT.Abs_reciprocal_sqrt)
 
-        bo_rows = const.tile([P, D], BF16)
-        nc.scalar.dma_start(out=bo_rows[:], in_=bo_l.partition_broadcast(P))
-        g_raw = const.tile([P, FEATURE_TILES], BF16)
-        nc.scalar.dma_start(
-            out=g_raw[:].rearrange("q (a e) -> q a e", e=PAIRS),
-            in_=g1.rearrange("(a q e) -> q a e", q=P, e=PAIRS),
-        )
-        be_raw = const.tile([P, FEATURE_TILES], BF16)
-        nc.scalar.dma_start(
-            out=be_raw[:].rearrange("q (a e) -> q a e", e=PAIRS),
-            in_=be1.rearrange("(a q e) -> q a e", q=P, e=PAIRS),
-        )
-
+        nc.sync.dma_start(out=bo_row[0:1, :], in_=bo_l.unsqueeze(0))
         wo_raw = keep.tile([P, FEATURE_TILES // PAIRS, PAIRS, D], BF16)
         wo_view = wo_l.rearrange("(a q e) k -> q a e k", q=P, e=PAIRS)
         for a in range(0, FEATURE_TILES // PAIRS, 2):
             nc.sync.dma_start(out=wo_raw[:, a : a + 2], in_=wo_view[:, a : a + 2])
         x_raw = keep.tile([P, TOKEN_TILES, D], BF16)
         wqkv_raw = []
-        for n in range(D3 // CHUNK):
+
+        def load_tokens_and_chunk(n):
             if 2 * n < TOKEN_TILES:
                 nc.sync.dma_start(out=x_raw[:, 2 * n : 2 * n + 2, :], in_=attn_l[:, 2 * n : 2 * n + 2, :])
             chunk_rows = stage.tile([P, ROW_TILES, D], BF16, tag="wqkv_raw", bufs=4)
@@ -83,18 +74,34 @@ def tile_hlgan_pb_kernel(tc, attn_l, wo_l, bo_l, g1, be1, wqkv_g, bqkv_g, out):
                 in_=wqkv_g[CHUNK * n : CHUNK * (n + 1), :].rearrange("(j p) k -> p j k", p=P),
             )
             wqkv_raw.append(chunk_rows)
+
+        load_tokens_and_chunk(0)
+        g_raw = const.tile([P, FEATURE_TILES], BF16)
+        nc.sync.dma_start(
+            out=g_raw[:].rearrange("q (a e) -> q a e", e=PAIRS),
+            in_=g1.rearrange("(a q e) -> q a e", q=P, e=PAIRS),
+        )
+        be_raw = const.tile([P, FEATURE_TILES], BF16)
+        nc.sync.dma_start(
+            out=be_raw[:].rearrange("q (a e) -> q a e", e=PAIRS),
+            in_=be1.rearrange("(a q e) -> q a e", q=P, e=PAIRS),
+        )
+        for n in range(1, D3 // CHUNK):
+            load_tokens_and_chunk(n)
         bqkv_rows = const.tile([P, D3], BF16)
         nc.sync.dma_start(out=bqkv_rows[:], in_=bqkv_g.partition_broadcast(P))
 
+        ones = const.tile([P, P], BF16)
+        nc.vector.memset(ones[:], 1.0)
         bo_cols = const.tile([P, D], BF16)
-        nc.gpsimd.tensor_scalar(
-            out=bo_cols[:].rearrange("p (a e q) -> p a e q", e=PAIRS, q=P),
-            in0=bo_rows[:].rearrange("p (a q e) -> p a e q", q=P, e=PAIRS),
-            scalar1=1.0,
-            scalar2=0.0,
-            op0=ALU.mult,
-            op1=ALU.add,
-        )
+        for h in range(D // CHUNK):
+            cols = slice(CHUNK * h, CHUNK * (h + 1))
+            acc = psum_acc.tile([P, CHUNK], F32, tag="acc")
+            nc.tensor.matmul(out=acc[:], lhsT=ones[:], rhs=bo_row[:, cols], start=True, stop=True)
+            nc.vector.tensor_copy(
+                out=bo_cols[:, cols].rearrange("p (a e q) -> p a e q", e=PAIRS, q=P),
+                in_=acc[:].rearrange("p (a q e) -> p a e q", q=P, e=PAIRS),
+            )
         gain = const.tile([P, FEATURE_TILES], F32)
         nc.gpsimd.tensor_copy(out=gain[:], in_=g_raw[:])
         shift = const.tile([P, FEATURE_TILES], F32)

@@ -49,7 +49,7 @@ def tile_hlgan_pb_kernel(tc, attn_l, wo_l, bo_l, g1, be1, wqkv_g, bqkv_g, out):
         ctx.enter_context(tc.manual_schedule())
 
         bo_row = const.tile([P, D], BF16)
-        nc.vector.memset(bo_row[:], 0.0)
+        nc.vector.memset(bo_row[:].bitcast(mybir.dt.int32), 0)
         ident = const.tile([P, P], F32)
         make_identity(nc, ident[:])
         eps = const.tile([P, 1], F32)
@@ -132,7 +132,7 @@ def tile_hlgan_pb_kernel(tc, attn_l, wo_l, bo_l, g1, be1, wqkv_g, bqkv_g, out):
             return 0 <= i < TOKEN_TILES
 
         w_grouped, x_grouped, y, y_sum, neg_mean, sum_sq = {}, {}, {}, {}, {}, {}
-        rstd, neg_mean_rstd, z, planes = {}, {}, {}, {}
+        rstd, neg_mean_rstd, z, planes, local_grouped = {}, {}, {}, {}, {}
 
         def transpose_weight_half(w, half, on_vector):
             rows, g = units[w][0], units[w][1]
@@ -260,11 +260,15 @@ def tile_hlgan_pb_kernel(tc, attn_l, wo_l, bo_l, g1, be1, wqkv_g, bqkv_g, out):
 
         def group_local(i):
             grouped = norm.tile([P, D], BF16, align_bytes=64, tag="local_grouped")
-            nc.vector.tensor_copy(
-                out=grouped[:].rearrange("q (g c i t) -> q g c t i", g=PASSES, i=4, t=PACK),
-                in_=planes[i][:].rearrange("q g t (c i) -> q g c t i", i=4),
+            nc.gpsimd.tensor_scalar(
+                out=grouped[:].rearrange("q (g r t) -> q g r t", g=PASSES, t=PACK),
+                in0=planes[i][:].rearrange("q g t r -> q g r t"),
+                scalar1=1.0,
+                scalar2=0.0,
+                op0=ALU.mult,
+                op1=ALU.add,
             )
-            return grouped
+            local_grouped[i] = grouped
 
         def qkv(i):
             for n in range(D3 // CHUNK):
@@ -305,15 +309,14 @@ def tile_hlgan_pb_kernel(tc, attn_l, wo_l, bo_l, g1, be1, wqkv_g, bqkv_g, out):
                 offset_step(r + NORM_AHEAD)
             if live(r + TURN_AHEAD):
                 turn_pass(r + TURN_AHEAD, 1)
+                group_local(r + TURN_AHEAD)
             if live(r + NORM_AHEAD):
                 normalise_step(r + NORM_AHEAD)
             if live(r):
                 qkv(r)
             if live(r + PROJECT_AHEAD):
                 project(r + PROJECT_AHEAD)
-            if live(r + TURN_AHEAD):
-                local_grouped = group_local(r + TURN_AHEAD)
             if live(r + TOKENS_AHEAD):
                 quantise_tile(x_grouped[r + TOKENS_AHEAD], x_codes, x_scales, r + TOKENS_AHEAD)
             if live(r + TURN_AHEAD):
-                quantise_tile(local_grouped, local_codes, local_scales, r + TURN_AHEAD)
+                quantise_tile(local_grouped[r + TURN_AHEAD], local_codes, local_scales, r + TURN_AHEAD)

@@ -25,12 +25,18 @@ CHUNK = 512
 ROW_TILES = CHUNK // P
 FEATURE_TILES = D // P
 
-TOKENS_AHEAD = 7
-PROJECT_AHEAD = 6
-NORM_AHEAD = 3
+NORM_AHEAD = 4
 TURN_AHEAD = 2
-UNITS_A_ROUND = 2
-FIRST_ROUND = -((D + D3) // CHUNK * PASSES // UNITS_A_ROUND)
+UNITS_A_ROUND = 3
+FIRST_ROUND = -(D3 // CHUNK * PASSES // UNITS_A_ROUND)
+X_EARLY = 4
+XORD = [[0, 1], [2], [3], [4], [], []]
+Y_BUFS = 8
+NORM_ON_G = True
+P_FIRST = False
+TURN_STEP = 0
+NORM_STEP = 2
+WV = ()
 
 FLOPS = 2 * P * TOKEN_TILES * D * (D + D3)
 
@@ -66,8 +72,8 @@ def tile_hlgan_pb_kernel(tc, attn_l, wo_l, bo_l, g1, be1, wqkv_g, bqkv_g, out):
         wqkv_raw = []
 
         def load_tokens_and_chunk(n):
-            if 2 * n < TOKEN_TILES:
-                nc.sync.dma_start(out=x_raw[:, 2 * n : 2 * n + 2, :], in_=attn_l[:, 2 * n : 2 * n + 2, :])
+            for m in XORD[n]:
+                nc.sync.dma_start(out=x_raw[:, 2 * m : 2 * m + 2, :], in_=attn_l[:, 2 * m : 2 * m + 2, :])
             chunk_rows = stage.tile([P, ROW_TILES, D], BF16, tag="wqkv_raw", bufs=4)
             nc.sync.dma_start(
                 out=chunk_rows[:],
@@ -152,7 +158,7 @@ def tile_hlgan_pb_kernel(tc, attn_l, wo_l, bo_l, g1, be1, wqkv_g, bqkv_g, out):
             else:
                 nc.scalar.copy(out=dst, in_=src)
 
-        def transpose_tokens(i):
+        def transpose_tokens(i, on_vector):
             x_words = x_raw[:, i, :].bitcast(F32)
             bank = psum_t.tile([P, PASSES, PAIRS, P], F32, tag="tp")
             for g in range(PASSES):
@@ -160,9 +166,10 @@ def tile_hlgan_pb_kernel(tc, attn_l, wo_l, bo_l, g1, be1, wqkv_g, bqkv_g, out):
                     first = WORDS_PER_PASS * g + P * u
                     nc.tensor.transpose(bank[:, g, u, :], x_words[:, first : first + P], ident[:])
             grouped = stage.tile([P, D], BF16, align_bytes=64, tag="x_grouped")
-            nc.scalar.copy(
-                out=grouped[:].bitcast(F32).rearrange("q (g r u) -> q g r u", g=PASSES, u=PAIRS),
-                in_=bank[:].rearrange("q g u r -> q g r u"),
+            copy_out(
+                grouped[:].bitcast(F32).rearrange("q (g r u) -> q g r u", g=PASSES, u=PAIRS),
+                bank[:].rearrange("q g u r -> q g r u"),
+                on_vector,
             )
             x_grouped[i] = grouped
 
@@ -186,7 +193,7 @@ def tile_hlgan_pb_kernel(tc, attn_l, wo_l, bo_l, g1, be1, wqkv_g, bqkv_g, out):
                 )
 
         def project(i):
-            in_flight = PROJECT_AHEAD - NORM_AHEAD + 2
+            in_flight = Y_BUFS
             y_tile = norm.tile([P, D], F32, tag="y", bufs=in_flight)
             sums = small.tile([P, D // CHUNK], F32, tag="y_sum", bufs=in_flight)
             for h in range(D // CHUNK):
@@ -235,9 +242,19 @@ def tile_hlgan_pb_kernel(tc, attn_l, wo_l, bo_l, g1, be1, wqkv_g, bqkv_g, out):
 
         def normalise_step(i):
             result = norm.tile([P, D], F32, tag="z", bufs=3)
-            nc.scalar.activation(
-                out=result[:], in_=y[i][:], func=ACT.Identity, bias=neg_mean_rstd[i][:], scale=rstd[i][:]
-            )
+            if NORM_ON_G:
+                nc.gpsimd.tensor_scalar(
+                    out=result[:],
+                    in0=y[i][:],
+                    scalar1=rstd[i][:],
+                    scalar2=neg_mean_rstd[i][:],
+                    op0=ALU.mult,
+                    op1=ALU.add,
+                )
+            else:
+                nc.scalar.activation(
+                    out=result[:], in_=y[i][:], func=ACT.Identity, bias=neg_mean_rstd[i][:], scale=rstd[i][:]
+                )
             z[i] = result
 
         def turn_pass(i, g):
@@ -279,44 +296,68 @@ def tile_hlgan_pb_kernel(tc, attn_l, wo_l, bo_l, g1, be1, wqkv_g, bqkv_g, out):
                 nc.vector.tensor_tensor(out=result[:], in0=acc[:], in1=bqkv_rows[:, cols], op=ALU.add)
                 nc.sync.dma_start(out=out[:, i, cols], in_=result[:])
 
-        copied = []
+        def copy_out(dst, src, on_vector):
+            if on_vector:
+                nc.vector.tensor_copy(out=dst, in_=src)
+            else:
+                nc.scalar.copy(out=dst, in_=src)
+
+        def quantise_unit(w):
+            nc.vector.quantize_mx(out=units[w][2].bitcast(FP8X4), scales=units[w][3], in_=w_grouped[w][:])
+
+        def quantise_x(i):
+            quantise_tile(x_grouped[i], x_codes, x_scales, i)
+
+        def quantise_local(i):
+            quantise_tile(local_grouped[i], local_codes, local_scales, i)
+
+        WO_UNITS = D // CHUNK * PASSES
+        for w in range(WO_UNITS):
+            transpose_weight_half(w, 0, False)
+            transpose_weight_half(w, 1, True)
+            if w > 0:
+                quantise_unit(w - 1)
+        for i in range(X_EARLY):
+            transpose_tokens(i, i % 2 == 1)
+            if i == 0:
+                quantise_unit(WO_UNITS - 1)
+            else:
+                quantise_x(i - 1)
+        todo = [(quantise_x, X_EARLY - 1)]
+
         for r in range(FIRST_ROUND, TOKEN_TILES):
-            for w in copied:
-                nc.vector.quantize_mx(
-                    out=units[w][2].bitcast(FP8X4), scales=units[w][3], in_=w_grouped[w][:]
-                )
-            copied = []
+            norm_i, turn_i = r + NORM_AHEAD, r + TURN_AHEAD
             if r < 0:
-                first_unit = UNITS_A_ROUND * (r - FIRST_ROUND)
-                copied = list(range(first_unit, first_unit + UNITS_A_ROUND))
-            for w in copied[:1]:
-                transpose_weight_half(w, 0, False)
-                transpose_weight_half(w, 1, live(r + NORM_AHEAD))
-            if live(r + NORM_AHEAD):
-                mean_step(r + NORM_AHEAD)
-            for w in copied[1:]:
-                transpose_weight_half(w, 0, False)
-                transpose_weight_half(w, 1, live(r + NORM_AHEAD))
-            if live(r + NORM_AHEAD):
-                squares_step(r + NORM_AHEAD)
-            if live(r + TOKENS_AHEAD):
-                transpose_tokens(r + TOKENS_AHEAD)
-            if live(r + NORM_AHEAD):
-                rstd_step(r + NORM_AHEAD)
-            if live(r + TURN_AHEAD):
-                turn_pass(r + TURN_AHEAD, 0)
-            if live(r + NORM_AHEAD):
-                offset_step(r + NORM_AHEAD)
-            if live(r + TURN_AHEAD):
-                turn_pass(r + TURN_AHEAD, 1)
-                group_local(r + TURN_AHEAD)
-            if live(r + NORM_AHEAD):
-                normalise_step(r + NORM_AHEAD)
+                steps = range(UNITS_A_ROUND)
+            else:
+                steps = range(1)
+            for s in steps:
+                for f, a in todo:
+                    f(a)
+                todo = []
+                if r < 0:
+                    n = UNITS_A_ROUND * (r - FIRST_ROUND) + s
+                    w = WO_UNITS + n
+                    if P_FIRST and live(n):
+                        project(n)
+                    transpose_weight_half(w, 0, False)
+                    transpose_weight_half(w, 1, s in WV)
+                    todo.append((quantise_unit, w))
+                    if live(n + X_EARLY):
+                        transpose_tokens(n + X_EARLY, False)
+                        todo.append((quantise_x, n + X_EARLY))
+                if r < 0 and not P_FIRST and live(n):
+                    project(n)
+                if s == min(TURN_STEP, steps[-1]) and live(turn_i):
+                    turn_pass(turn_i, 0)
+                    turn_pass(turn_i, 1)
+                    group_local(turn_i)
+                    todo.append((quantise_local, turn_i))
+                if s == min(NORM_STEP, steps[-1]) and live(norm_i) and r > FIRST_ROUND or s == steps[-1] and r == FIRST_ROUND:
+                    mean_step(norm_i)
+                    squares_step(norm_i)
+                    rstd_step(norm_i)
+                    offset_step(norm_i)
+                    normalise_step(norm_i)
             if live(r):
                 qkv(r)
-            if live(r + PROJECT_AHEAD):
-                project(r + PROJECT_AHEAD)
-            if live(r + TOKENS_AHEAD):
-                quantise_tile(x_grouped[r + TOKENS_AHEAD], x_codes, x_scales, r + TOKENS_AHEAD)
-            if live(r + TURN_AHEAD):
-                quantise_tile(local_grouped[r + TURN_AHEAD], local_codes, local_scales, r + TURN_AHEAD)

@@ -5,6 +5,7 @@ from concourse.masks import make_identity
 
 F32 = mybir.dt.float32
 BF16 = mybir.dt.bfloat16
+I32 = mybir.dt.int32
 U32 = mybir.dt.uint32
 U8 = mybir.dt.uint8
 FP8X4 = mybir.dt.float8_e4m3fn_x4
@@ -24,19 +25,31 @@ WORDS_PER_PASS = K_PASS // PAIRS
 CHUNK = 512
 ROW_TILES = CHUNK // P
 FEATURE_TILES = D // P
+WO_CHUNKS = D // CHUNK
+OUT_CHUNKS = D3 // CHUNK
+WO_UNITS = WO_CHUNKS * PASSES
 
 NORM_AHEAD = 4
 TURN_AHEAD = 2
+TURN_PAIR = 1
 UNITS_A_ROUND = 3
-FIRST_ROUND = -(D3 // CHUNK * PASSES // UNITS_A_ROUND)
+FIRST_ROUND = -(OUT_CHUNKS * PASSES // UNITS_A_ROUND)
 X_EARLY = 4
-XORD = [[0, 1], [2], [3], [4], [], []]
-Y_BUFS = 8
-NORM_ON_G = True
-P_FIRST = False
+P_LEAD = 1
 TURN_STEP = 0
 NORM_STEP = 2
-WV = ()
+W_BUFS = 5
+Y_BUFS = 8
+Z_BUFS = 4
+OUT_BUFS = 8
+T_BANKS = 4
+WV = (0,)
+WO_V = (1, 3)
+XH_V = (1,)
+OG = ()
+NORM_G = True
+XORD = [[0, 1], [2], [3], [4], [], []]
+OG_ADD_LATE = 1
 
 FLOPS = 2 * P * TOKEN_TILES * D * (D + D3)
 
@@ -49,69 +62,59 @@ def tile_hlgan_pb_kernel(tc, attn_l, wo_l, bo_l, g1, be1, wqkv_g, bqkv_g, out):
         stage = ctx.enter_context(tc.tile_pool(name="stage", bufs=2))
         norm = ctx.enter_context(tc.tile_pool(name="norm", bufs=2))
         small = ctx.enter_context(tc.tile_pool(name="small", bufs=2))
-        out_pool = ctx.enter_context(tc.tile_pool(name="out_pool", bufs=8))
-        psum_t = ctx.enter_context(tc.psum_pool(name="psum_t", bufs=5))
-        psum_acc = ctx.enter_context(tc.psum_pool(name="psum_acc", bufs=3))
+        out_pool = ctx.enter_context(tc.tile_pool(name="out_pool", bufs=OUT_BUFS))
+        psum_t = ctx.enter_context(tc.psum_pool(name="psum_t", bufs=T_BANKS))
+        psum_acc = ctx.enter_context(tc.psum_pool(name="psum_acc", bufs=8 - T_BANKS))
         ctx.enter_context(tc.manual_schedule())
 
+        w_rows = []
+        wo_view = wo_l.rearrange("(a q e) k -> q a e k", q=P, e=PAIRS)
+        for h in range(WO_CHUNKS):
+            rows = stage.tile([P, ROW_TILES, D], BF16, tag="w_rows", bufs=W_BUFS)
+            for a in range(ROW_TILES // PAIRS):
+                nc.sync.dma_start(
+                    out=rows[:, PAIRS * a : PAIRS * (a + 1)], in_=wo_view[:, ROW_TILES // PAIRS * h + a]
+                )
+            w_rows.append(rows)
         bo_row = const.tile([P, D], BF16)
-        nc.vector.memset(bo_row[:].bitcast(mybir.dt.int32), 0)
+        nc.vector.memset(bo_row[:].bitcast(I32), 0)
+        nc.sync.dma_start(out=bo_row[0:1, :], in_=bo_l.unsqueeze(0))
+        x_raw = keep.tile([P, TOKEN_TILES, D], BF16)
+        g_raw = const.tile([P, FEATURE_TILES], BF16)
+        be_raw = const.tile([P, FEATURE_TILES], BF16)
+        for n in range(OUT_CHUNKS):
+            for m in XORD[n]:
+                nc.sync.dma_start(out=x_raw[:, 2 * m : 2 * m + 2, :], in_=attn_l[:, 2 * m : 2 * m + 2, :])
+            rows = stage.tile([P, ROW_TILES, D], BF16, tag="w_rows", bufs=W_BUFS)
+            nc.sync.dma_start(
+                out=rows[:], in_=wqkv_g[CHUNK * n : CHUNK * (n + 1), :].rearrange("(j p) k -> p j k", p=P)
+            )
+            w_rows.append(rows)
+            if n == 0:
+                nc.sync.dma_start(
+                    out=g_raw[:].rearrange("q (a e) -> q a e", e=PAIRS),
+                    in_=g1.rearrange("(a q e) -> q a e", q=P, e=PAIRS),
+                )
+                nc.sync.dma_start(
+                    out=be_raw[:].rearrange("q (a e) -> q a e", e=PAIRS),
+                    in_=be1.rearrange("(a q e) -> q a e", q=P, e=PAIRS),
+                )
+        bqkv_rows = const.tile([P, D3], BF16)
+        nc.sync.dma_start(out=bqkv_rows[:], in_=bqkv_g.partition_broadcast(P))
+
         ident = const.tile([P, P], F32)
         make_identity(nc, ident[:])
+        ones = const.tile([P, P], BF16)
+        nc.vector.memset(ones[:], 1.0)
         eps = const.tile([P, 1], F32)
         nc.vector.memset(eps[:], EPS)
         warm = const.tile([P, 1], F32)
         nc.scalar.activation(out=warm[:], in_=eps[:], func=ACT.Abs_reciprocal_sqrt)
-
-        nc.sync.dma_start(out=bo_row[0:1, :], in_=bo_l.unsqueeze(0))
-        wo_raw = keep.tile([P, FEATURE_TILES // PAIRS, PAIRS, D], BF16)
-        wo_view = wo_l.rearrange("(a q e) k -> q a e k", q=P, e=PAIRS)
-        for a in range(0, FEATURE_TILES // PAIRS, 2):
-            nc.sync.dma_start(out=wo_raw[:, a : a + 2], in_=wo_view[:, a : a + 2])
-        x_raw = keep.tile([P, TOKEN_TILES, D], BF16)
-        wqkv_raw = []
-
-        def load_tokens_and_chunk(n):
-            for m in XORD[n]:
-                nc.sync.dma_start(out=x_raw[:, 2 * m : 2 * m + 2, :], in_=attn_l[:, 2 * m : 2 * m + 2, :])
-            chunk_rows = stage.tile([P, ROW_TILES, D], BF16, tag="wqkv_raw", bufs=4)
-            nc.sync.dma_start(
-                out=chunk_rows[:],
-                in_=wqkv_g[CHUNK * n : CHUNK * (n + 1), :].rearrange("(j p) k -> p j k", p=P),
-            )
-            wqkv_raw.append(chunk_rows)
-
-        load_tokens_and_chunk(0)
-        g_raw = const.tile([P, FEATURE_TILES], BF16)
-        nc.sync.dma_start(
-            out=g_raw[:].rearrange("q (a e) -> q a e", e=PAIRS),
-            in_=g1.rearrange("(a q e) -> q a e", q=P, e=PAIRS),
-        )
-        be_raw = const.tile([P, FEATURE_TILES], BF16)
-        nc.sync.dma_start(
-            out=be_raw[:].rearrange("q (a e) -> q a e", e=PAIRS),
-            in_=be1.rearrange("(a q e) -> q a e", q=P, e=PAIRS),
-        )
-        for n in range(1, D3 // CHUNK):
-            load_tokens_and_chunk(n)
-        bqkv_rows = const.tile([P, D3], BF16)
-        nc.sync.dma_start(out=bqkv_rows[:], in_=bqkv_g.partition_broadcast(P))
-
-        ones = const.tile([P, P], BF16)
-        nc.vector.memset(ones[:], 1.0)
-        bo_cols = const.tile([P, D], BF16)
-        for h in range(D // CHUNK):
-            cols = slice(CHUNK * h, CHUNK * (h + 1))
-            acc = psum_acc.tile([P, CHUNK], F32, tag="acc")
-            nc.tensor.matmul(out=acc[:], lhsT=ones[:], rhs=bo_row[:, cols], start=True, stop=True)
-            nc.vector.tensor_copy(
-                out=bo_cols[:, cols].rearrange("p (a e q) -> p a e q", e=PAIRS, q=P),
-                in_=acc[:].rearrange("p (a q e) -> p a e q", q=P, e=PAIRS),
-            )
         gain = const.tile([P, FEATURE_TILES], F32)
         nc.gpsimd.tensor_copy(out=gain[:], in_=g_raw[:])
         shift = const.tile([P, FEATURE_TILES], F32)
         nc.gpsimd.tensor_copy(out=shift[:], in_=be_raw[:])
+        bo_cols = const.tile([P, D], BF16)
 
         x_codes = keep.tile([P, TOKEN_TILES, PASSES, P], U32, align_bytes=64)
         x_scales = keep.tile([P, TOKEN_TILES, PASSES, P], U8, align_bytes=64)
@@ -123,27 +126,32 @@ def tile_hlgan_pb_kernel(tc, attn_l, wo_l, bo_l, g1, be1, wqkv_g, bqkv_g, out):
         wqkv_scales = keep.tile([P, PASSES, D3], U8, align_bytes=64)
 
         units = []
-        for h in range(D // CHUNK):
-            cols = slice(CHUNK * h, CHUNK * (h + 1))
-            rows = [wo_raw[:, 2 * h + j // 2, j % 2, :].bitcast(F32) for j in range(ROW_TILES)]
+        for n in range(WO_CHUNKS + OUT_CHUNKS):
+            if n < WO_CHUNKS:
+                codes, scales, first_col = wo_codes, wo_scales, CHUNK * n
+            else:
+                codes, scales, first_col = wqkv_codes, wqkv_scales, CHUNK * (n - WO_CHUNKS)
+            cols = slice(first_col, first_col + CHUNK)
+            rows = [w_rows[n][:, j, :].bitcast(F32) for j in range(ROW_TILES)]
             for g in range(PASSES):
-                units.append((rows, g, wo_codes[:, g, cols], wo_scales[:, g, cols]))
-        for n in range(D3 // CHUNK):
-            cols = slice(CHUNK * n, CHUNK * (n + 1))
-            rows = [wqkv_raw[n][:, j, :].bitcast(F32) for j in range(ROW_TILES)]
-            for g in range(PASSES):
-                units.append((rows, g, wqkv_codes[:, g, cols], wqkv_scales[:, g, cols]))
+                units.append((rows, g, codes[:, g, cols], scales[:, g, cols]))
 
         def live(i):
             return 0 <= i < TOKEN_TILES
 
+        def copy_out(dst, src, on_vector):
+            if on_vector:
+                nc.vector.tensor_copy(out=dst, in_=src)
+            else:
+                nc.scalar.copy(out=dst, in_=src)
+
         w_grouped, x_grouped, y, y_sum, neg_mean, sum_sq = {}, {}, {}, {}, {}, {}
         rstd, neg_mean_rstd, z, planes, local_grouped = {}, {}, {}, {}, {}
 
-        def transpose_weight_half(w, half, on_vector):
+        def transpose_unit_half(w, half, on_vector):
             rows, g = units[w][0], units[w][1]
             if half == 0:
-                grouped = stage.tile([P, PACK * CHUNK], BF16, align_bytes=64, tag="w_grouped", bufs=4)
+                grouped = stage.tile([P, PACK * CHUNK], BF16, align_bytes=64, tag="w_grouped", bufs=3)
                 w_grouped[w] = grouped
             bank = psum_t.tile([P, PAIRS, 2, P], F32, tag="tp")
             for u in range(PAIRS):
@@ -151,12 +159,11 @@ def tile_hlgan_pb_kernel(tc, attn_l, wo_l, bo_l, g1, be1, wqkv_g, bqkv_g, out):
                 for j in range(2):
                     nc.tensor.transpose(bank[:, u, j, :], rows[2 * half + j][:, first : first + P], ident[:])
             words = w_grouped[w][:].bitcast(F32).rearrange("q (n u) -> q n u", u=PAIRS)
-            dst = words[:, 2 * P * half : 2 * P * (half + 1), :]
-            src = bank[:].rearrange("q u j r -> q (j r) u")
-            if on_vector:
-                nc.vector.tensor_copy(out=dst, in_=src)
-            else:
-                nc.scalar.copy(out=dst, in_=src)
+            copy_out(
+                words[:, 2 * P * half : 2 * P * (half + 1), :],
+                bank[:].rearrange("q u j r -> q (j r) u"),
+                on_vector,
+            )
 
         def transpose_tokens(i, on_vector):
             x_words = x_raw[:, i, :].bitcast(F32)
@@ -173,12 +180,31 @@ def tile_hlgan_pb_kernel(tc, attn_l, wo_l, bo_l, g1, be1, wqkv_g, bqkv_g, out):
             )
             x_grouped[i] = grouped
 
+        def spread_bias():
+            for h in range(WO_CHUNKS):
+                cols = slice(CHUNK * h, CHUNK * (h + 1))
+                acc = psum_acc.tile([P, CHUNK], F32, tag="acc")
+                nc.tensor.matmul(out=acc[:], lhsT=ones[:], rhs=bo_row[:, cols], start=True, stop=True)
+                nc.scalar.copy(
+                    out=bo_cols[:, cols].rearrange("p (a e q) -> p a e q", e=PAIRS, q=P),
+                    in_=acc[:].rearrange("p (a q e) -> p a e q", q=P, e=PAIRS),
+                )
+
+        def quantise_unit(w):
+            nc.vector.quantize_mx(out=units[w][2].bitcast(FP8X4), scales=units[w][3], in_=w_grouped[w][:])
+
         def quantise_tile(grouped, codes, scales, i):
             nc.vector.quantize_mx(
                 out=codes[:, i].rearrange("q g r -> q (g r)").bitcast(FP8X4),
                 scales=scales[:, i].rearrange("q g r -> q (g r)"),
                 in_=grouped[:],
             )
+
+        def quantise_tokens(i):
+            quantise_tile(x_grouped[i], x_codes, x_scales, i)
+
+        def quantise_local(i):
+            quantise_tile(local_grouped[i], local_codes, local_scales, i)
 
         def multiply(acc, a_codes, a_scales, i, b_codes, b_scales, cols):
             for g in range(PASSES):
@@ -193,10 +219,9 @@ def tile_hlgan_pb_kernel(tc, attn_l, wo_l, bo_l, g1, be1, wqkv_g, bqkv_g, out):
                 )
 
         def project(i):
-            in_flight = Y_BUFS
-            y_tile = norm.tile([P, D], F32, tag="y", bufs=in_flight)
-            sums = small.tile([P, D // CHUNK], F32, tag="y_sum", bufs=in_flight)
-            for h in range(D // CHUNK):
+            y_tile = norm.tile([P, D], F32, tag="y", bufs=Y_BUFS)
+            sums = small.tile([P, WO_CHUNKS], F32, tag="y_sum", bufs=Y_BUFS)
+            for h in range(WO_CHUNKS):
                 cols = slice(CHUNK * h, CHUNK * (h + 1))
                 acc = psum_acc.tile([P, CHUNK], F32, tag="acc")
                 multiply(acc, x_codes, x_scales, i, wo_codes, wo_scales, cols)
@@ -212,74 +237,52 @@ def tile_hlgan_pb_kernel(tc, attn_l, wo_l, bo_l, g1, be1, wqkv_g, bqkv_g, out):
             y[i] = y_tile
             y_sum[i] = sums
 
-        def mean_step(i):
-            scaled = small.tile([P, D // CHUNK], F32, tag="scaled")
-            result = small.tile([P, 1], F32, tag="neg_mean")
+        def normalise(i):
+            scaled = small.tile([P, WO_CHUNKS], F32, tag="scaled")
+            neg_mean = small.tile([P, 1], F32, tag="neg_mean")
             nc.scalar.activation(
-                out=scaled[:], in_=y_sum[i][:], func=ACT.Copy, scale=-1.0 / D, accum_out=result[:]
+                out=scaled[:], in_=y_sum[i][:], func=ACT.Copy, scale=-1.0 / D, accum_out=neg_mean[:]
             )
-            neg_mean[i] = result
-
-        def squares_step(i):
             squares = norm.tile([P, D], BF16, tag="squares", bufs=1)
-            result = small.tile([P, 1], F32, tag="sum_sq")
+            sum_sq = small.tile([P, 1], F32, tag="sum_sq")
             nc.scalar.activation(
-                out=squares[:], in_=y[i][:], func=ACT.Square, bias=neg_mean[i][:], accum_out=result[:]
+                out=squares[:], in_=y[i][:], func=ACT.Square, bias=neg_mean[:], accum_out=sum_sq[:]
             )
-            sum_sq[i] = result
-
-        def rstd_step(i):
-            result = small.tile([P, 1], F32, tag="rstd")
+            rstd = small.tile([P, 1], F32, tag="rstd")
             nc.scalar.activation(
-                out=result[:], in_=sum_sq[i][:], func=ACT.Abs_reciprocal_sqrt, bias=eps[:], scale=1.0 / D
+                out=rstd[:], in_=sum_sq[:], func=ACT.Abs_reciprocal_sqrt, bias=eps[:], scale=1.0 / D
             )
-            rstd[i] = result
-
-        def offset_step(i):
-            result = small.tile([P, 1], F32, tag="neg_mean_rstd")
-            nc.scalar.mul(out=result[:], in_=neg_mean[i][:], mul=rstd[i][:])
-            neg_mean_rstd[i] = result
-
-        def normalise_step(i):
-            result = norm.tile([P, D], F32, tag="z", bufs=3)
-            if NORM_ON_G:
+            offset = small.tile([P, 1], F32, tag="offset")
+            nc.scalar.mul(out=offset[:], in_=neg_mean[:], mul=rstd[:])
+            result = norm.tile([P, D], F32, tag="z", bufs=Z_BUFS)
+            if NORM_G:
                 nc.gpsimd.tensor_scalar(
-                    out=result[:],
-                    in0=y[i][:],
-                    scalar1=rstd[i][:],
-                    scalar2=neg_mean_rstd[i][:],
-                    op0=ALU.mult,
-                    op1=ALU.add,
+                    out=result[:], in0=y[i][:], scalar1=rstd[:], scalar2=offset[:], op0=ALU.mult, op1=ALU.add
                 )
             else:
-                nc.scalar.activation(
-                    out=result[:], in_=y[i][:], func=ACT.Identity, bias=neg_mean_rstd[i][:], scale=rstd[i][:]
-                )
+                nc.scalar.activation(out=result[:], in_=y[i][:], func=ACT.Identity, bias=offset[:], scale=rstd[:])
             z[i] = result
 
-        def turn_pass(i, g):
-            if g == 0:
-                tile_planes = norm.tile([P, PASSES, PACK, P], BF16, tag="planes")
-                planes[i] = tile_planes
-            bank = psum_t.tile([P, PACK, P], F32, tag="tp")
-            for t in range(PACK):
-                j = PACK * g + t
-                nc.tensor.transpose(bank[:, t, :], z[i][:, P * j : P * (j + 1)], ident[:])
-            for t in range(PACK):
-                j = PACK * g + t
-                nc.scalar.activation(
-                    out=planes[i][:, g, t, :],
-                    in_=bank[:, t, :],
-                    func=ACT.Identity,
-                    bias=shift[:, j : j + 1],
-                    scale=gain[:, j : j + 1],
-                )
-
-        def group_local(i):
+        def turn(i):
+            tile_planes = norm.tile([P, PASSES, PACK, P], BF16, tag="planes")
+            for g in range(PASSES):
+                bank = psum_t.tile([P, PACK, P], F32, tag="tp")
+                for t in range(PACK):
+                    j = PACK * g + t
+                    nc.tensor.transpose(bank[:, t, :], z[i][:, P * j : P * (j + 1)], ident[:])
+                for t in range(PACK):
+                    j = PACK * g + t
+                    nc.scalar.activation(
+                        out=tile_planes[:, g, t, :],
+                        in_=bank[:, t, :],
+                        func=ACT.Identity,
+                        bias=shift[:, j : j + 1],
+                        scale=gain[:, j : j + 1],
+                    )
             grouped = norm.tile([P, D], BF16, align_bytes=64, tag="local_grouped")
             nc.gpsimd.tensor_scalar(
                 out=grouped[:].rearrange("q (g r t) -> q g r t", g=PASSES, t=PACK),
-                in0=planes[i][:].rearrange("q g t r -> q g r t"),
+                in0=tile_planes[:].rearrange("q g t r -> q g r t"),
                 scalar1=1.0,
                 scalar2=0.0,
                 op0=ALU.mult,
@@ -288,76 +291,65 @@ def tile_hlgan_pb_kernel(tc, attn_l, wo_l, bo_l, g1, be1, wqkv_g, bqkv_g, out):
             local_grouped[i] = grouped
 
         def qkv(i):
-            for n in range(D3 // CHUNK):
+            for n in range(OUT_CHUNKS):
                 cols = slice(CHUNK * n, CHUNK * (n + 1))
                 acc = psum_acc.tile([P, CHUNK], F32, tag="acc")
                 multiply(acc, local_codes, local_scales, i, wqkv_codes, wqkv_scales, cols)
                 result = out_pool.tile([P, CHUNK], F32, tag="result")
-                nc.vector.tensor_tensor(out=result[:], in0=acc[:], in1=bqkv_rows[:, cols], op=ALU.add)
+                if n in OG and i < TOKEN_TILES - 1:
+                    raw = out_pool.tile([P, CHUNK], F32, tag="raw", bufs=2)
+                    nc.scalar.copy(out=raw[:], in_=acc[:])
+                    nc.gpsimd.tensor_tensor(out=result[:], in0=raw[:], in1=bqkv_rows[:, cols], op=ALU.add)
+                else:
+                    nc.vector.tensor_tensor(out=result[:], in0=acc[:], in1=bqkv_rows[:, cols], op=ALU.add)
                 nc.sync.dma_start(out=out[:, i, cols], in_=result[:])
 
-        def copy_out(dst, src, on_vector):
-            if on_vector:
-                nc.vector.tensor_copy(out=dst, in_=src)
+        for h in range(WO_CHUNKS):
+            pair = range(PASSES * h, PASSES * (h + 1))
+            for half in range(2):
+                for w in pair:
+                    transpose_unit_half(w, half, 4 * h + 2 * half + w % 2 in WO_V)
+            if h == 0:
+                for w in pair:
+                    quantise_unit(w)
             else:
-                nc.scalar.copy(out=dst, in_=src)
-
-        def quantise_unit(w):
-            nc.vector.quantize_mx(out=units[w][2].bitcast(FP8X4), scales=units[w][3], in_=w_grouped[w][:])
-
-        def quantise_x(i):
-            quantise_tile(x_grouped[i], x_codes, x_scales, i)
-
-        def quantise_local(i):
-            quantise_tile(local_grouped[i], local_codes, local_scales, i)
-
-        WO_UNITS = D // CHUNK * PASSES
-        for w in range(WO_UNITS):
-            transpose_weight_half(w, 0, False)
-            transpose_weight_half(w, 1, True)
-            if w > 0:
-                quantise_unit(w - 1)
+                quantise_unit(pair[0])
+        spread_bias()
         for i in range(X_EARLY):
-            transpose_tokens(i, i % 2 == 1)
+            transpose_tokens(i, i in XH_V)
             if i == 0:
                 quantise_unit(WO_UNITS - 1)
             else:
-                quantise_x(i - 1)
-        todo = [(quantise_x, X_EARLY - 1)]
+                quantise_tokens(i - 1)
+        quantise_tokens(X_EARLY - 1)
+        for i in range(P_LEAD):
+            project(i)
 
+        todo = []
         for r in range(FIRST_ROUND, TOKEN_TILES):
             norm_i, turn_i = r + NORM_AHEAD, r + TURN_AHEAD
-            if r < 0:
-                steps = range(UNITS_A_ROUND)
-            else:
-                steps = range(1)
-            for s in steps:
+            for s in range(UNITS_A_ROUND if r < 0 else 1):
+                last = r >= 0 or s == UNITS_A_ROUND - 1
                 for f, a in todo:
                     f(a)
                 todo = []
+                if (r >= 0 or s == TURN_STEP) and turn_i % TURN_PAIR == 0:
+                    for i in range(turn_i, turn_i + TURN_PAIR):
+                        if live(i):
+                            turn(i)
+                            todo.append((quantise_local, i))
                 if r < 0:
                     n = UNITS_A_ROUND * (r - FIRST_ROUND) + s
                     w = WO_UNITS + n
-                    if P_FIRST and live(n):
-                        project(n)
-                    transpose_weight_half(w, 0, False)
-                    transpose_weight_half(w, 1, s in WV)
+                    transpose_unit_half(w, 0, False)
+                    transpose_unit_half(w, 1, s in WV)
                     todo.append((quantise_unit, w))
                     if live(n + X_EARLY):
                         transpose_tokens(n + X_EARLY, False)
-                        todo.append((quantise_x, n + X_EARLY))
-                if r < 0 and not P_FIRST and live(n):
-                    project(n)
-                if s == min(TURN_STEP, steps[-1]) and live(turn_i):
-                    turn_pass(turn_i, 0)
-                    turn_pass(turn_i, 1)
-                    group_local(turn_i)
-                    todo.append((quantise_local, turn_i))
-                if s == min(NORM_STEP, steps[-1]) and live(norm_i) and r > FIRST_ROUND or s == steps[-1] and r == FIRST_ROUND:
-                    mean_step(norm_i)
-                    squares_step(norm_i)
-                    rstd_step(norm_i)
-                    offset_step(norm_i)
-                    normalise_step(norm_i)
+                        todo.append((quantise_tokens, n + X_EARLY))
+                    if live(n + P_LEAD):
+                        project(n + P_LEAD)
+                if live(norm_i) and (r >= 0 or s == (UNITS_A_ROUND - 1 if r == FIRST_ROUND else NORM_STEP)):
+                    normalise(norm_i)
             if live(r):
                 qkv(r)

@@ -116,14 +116,14 @@ def tile_hlgan_pb_kernel(tc, attn_l, wo_l, bo_l, g1, be1, wqkv_g, bqkv_g, out):
         nc.gpsimd.tensor_copy(out=shift[:], in_=be_raw[:])
         bo_cols = const.tile([P, D], BF16)
 
-        x_codes = keep.tile([P, TOKEN_TILES, PASSES, P], U32, align_bytes=64)
-        x_scales = keep.tile([P, TOKEN_TILES, PASSES, P], U8, align_bytes=64)
-        wo_codes = keep.tile([P, PASSES, D], U32, align_bytes=64)
-        wo_scales = keep.tile([P, PASSES, D], U8, align_bytes=64)
-        local_codes = keep.tile([P, TOKEN_TILES, PASSES, P], U32, align_bytes=64)
-        local_scales = keep.tile([P, TOKEN_TILES, PASSES, P], U8, align_bytes=64)
-        wqkv_codes = keep.tile([P, PASSES, D3], U32, align_bytes=64)
-        wqkv_scales = keep.tile([P, PASSES, D3], U8, align_bytes=64)
+        x_codes = keep.tile([P, TOKEN_TILES, PASSES, P], U32, align_bytes=256)
+        x_scales = keep.tile([P, TOKEN_TILES, PASSES, P], U8, align_bytes=256)
+        wo_codes = keep.tile([P, PASSES, D], U32, align_bytes=256)
+        wo_scales = keep.tile([P, PASSES, D], U8, align_bytes=256)
+        local_codes = keep.tile([P, TOKEN_TILES, PASSES, P], U32, align_bytes=256)
+        local_scales = keep.tile([P, TOKEN_TILES, PASSES, P], U8, align_bytes=256)
+        wqkv_codes = keep.tile([P, PASSES, D3], U32, align_bytes=256)
+        wqkv_scales = keep.tile([P, PASSES, D3], U8, align_bytes=256)
 
         units = []
         for n in range(WO_CHUNKS + OUT_CHUNKS):

@@ -32,12 +32,18 @@ WO_UNITS = WO_CHUNKS * PASSES
 NORM_AHEAD = 4
 TURN_AHEAD = 2
 TURN_PAIR = 1
-UNITS_A_ROUND = 3
-FIRST_ROUND = -(OUT_CHUNKS * PASSES // UNITS_A_ROUND)
+UNITS_A_ROUND = 2
+LATE_FIRST = False
+FIRST_ROUND = -5
+NORM_LAST_FIRST = False
 X_EARLY = 4
 P_LEAD = 1
+Q_POS = 9
+WV_IDLE = False
+X_AFTER = 5
+HEAD = 1
 TURN_STEP = 0
-NORM_STEP = 2
+NORM_STEP = 1
 W_BUFS = 5
 Y_BUFS = 8
 Z_BUFS = 4
@@ -69,7 +75,10 @@ def tile_hlgan_pb_kernel(tc, attn_l, wo_l, bo_l, g1, be1, wqkv_g, bqkv_g, out):
 
         w_rows = []
         wo_view = wo_l.rearrange("(a q e) k -> q a e k", q=P, e=PAIRS)
+        x_raw = keep.tile([P, TOKEN_TILES, D], BF16)
         for h in range(WO_CHUNKS):
+            if h == X_AFTER:
+                nc.sync.dma_start(out=x_raw[:, 0:2, :], in_=attn_l[:, 0:2, :])
             rows = stage.tile([P, ROW_TILES, D], BF16, tag="w_rows", bufs=W_BUFS)
             for a in range(ROW_TILES // PAIRS):
                 nc.sync.dma_start(
@@ -79,11 +88,12 @@ def tile_hlgan_pb_kernel(tc, attn_l, wo_l, bo_l, g1, be1, wqkv_g, bqkv_g, out):
         bo_row = const.tile([P, D], BF16)
         nc.vector.memset(bo_row[:].bitcast(I32), 0)
         nc.sync.dma_start(out=bo_row[0:1, :], in_=bo_l.unsqueeze(0))
-        x_raw = keep.tile([P, TOKEN_TILES, D], BF16)
         g_raw = const.tile([P, FEATURE_TILES], BF16)
         be_raw = const.tile([P, FEATURE_TILES], BF16)
         for n in range(OUT_CHUNKS):
             for m in XORD[n]:
+                if m == 0 and X_AFTER == 1:
+                    continue
                 nc.sync.dma_start(out=x_raw[:, 2 * m : 2 * m + 2, :], in_=attn_l[:, 2 * m : 2 * m + 2, :])
             rows = stage.tile([P, ROW_TILES, D], BF16, tag="w_rows", bufs=W_BUFS)
             nc.sync.dma_start(
@@ -290,8 +300,21 @@ def tile_hlgan_pb_kernel(tc, attn_l, wo_l, bo_l, g1, be1, wqkv_g, bqkv_g, out):
             )
             local_grouped[i] = grouped
 
-        def qkv(i):
-            for n in range(OUT_CHUNKS):
+        early_units = UNITS_A_ROUND * -FIRST_ROUND
+
+        def ready_round(n):
+            return max(0, PASSES * (n + 1) - early_units)
+
+        def products(r):
+            late = [(i, n) for n in range(OUT_CHUNKS) if 0 < ready_round(n) == r for i in range(r)]
+            own = [(r, n) for n in range(OUT_CHUNKS) if ready_round(n) <= r]
+            return late + own if LATE_FIRST else own + late
+
+        def qkv(pairs, after):
+            for count, (i, n) in enumerate(pairs):
+                if count == Q_POS:
+                    for f, a in after:
+                        f(a)
                 cols = slice(CHUNK * n, CHUNK * (n + 1))
                 acc = psum_acc.tile([P, CHUNK], F32, tag="acc")
                 multiply(acc, local_codes, local_scales, i, wqkv_codes, wqkv_scales, cols)
@@ -304,28 +327,54 @@ def tile_hlgan_pb_kernel(tc, attn_l, wo_l, bo_l, g1, be1, wqkv_g, bqkv_g, out):
                     nc.vector.tensor_tensor(out=result[:], in0=acc[:], in1=bqkv_rows[:, cols], op=ALU.add)
                 nc.sync.dma_start(out=out[:, i, cols], in_=result[:])
 
-        for h in range(WO_CHUNKS):
-            pair = range(PASSES * h, PASSES * (h + 1))
+        def unit_pair(h):
             for half in range(2):
-                for w in pair:
-                    transpose_unit_half(w, half, 4 * h + 2 * half + w % 2 in WO_V)
-            if h == 0:
-                for w in pair:
-                    quantise_unit(w)
-            else:
-                quantise_unit(pair[0])
-        spread_bias()
-        for i in range(X_EARLY):
-            transpose_tokens(i, i in XH_V)
-            if i == 0:
-                quantise_unit(WO_UNITS - 1)
-            else:
-                quantise_tokens(i - 1)
-        quantise_tokens(X_EARLY - 1)
-        for i in range(P_LEAD):
-            project(i)
+                for g in range(PASSES):
+                    transpose_unit_half(PASSES * h + g, half, 4 * h + 2 * half + g in WO_V)
 
-        todo = []
+        if HEAD == 0:
+            unit_pair(0)
+            for i in range(2):
+                transpose_tokens(i, i in XH_V)
+            quantise_unit(0)
+            quantise_unit(1)
+            spread_bias()
+            quantise_tokens(0)
+            quantise_tokens(1)
+            unit_pair(1)
+            quantise_unit(2)
+            quantise_unit(3)
+            todo = []
+            for i in range(2, X_EARLY):
+                transpose_tokens(i, i in XH_V)
+                todo.append((quantise_tokens, i))
+            for i in range(P_LEAD):
+                project(i)
+        else:
+            unit_pair(0)
+            quantise_unit(0)
+            quantise_unit(1)
+            unit_pair(1)
+            for i in range(2):
+                transpose_tokens(i, i in XH_V)
+            spread_bias()
+            if HEAD == 1:
+                quantise_tokens(0)
+                quantise_unit(2)
+                quantise_unit(3)
+                quantise_tokens(1)
+            else:
+                quantise_unit(2)
+                quantise_unit(3)
+                quantise_tokens(0)
+                quantise_tokens(1)
+            todo = []
+            for i in range(2, X_EARLY):
+                transpose_tokens(i, i in XH_V)
+                todo.append((quantise_tokens, i))
+            for i in range(P_LEAD):
+                project(i)
+
         for r in range(FIRST_ROUND, TOKEN_TILES):
             norm_i, turn_i = r + NORM_AHEAD, r + TURN_AHEAD
             for s in range(UNITS_A_ROUND if r < 0 else 1):
@@ -333,23 +382,27 @@ def tile_hlgan_pb_kernel(tc, attn_l, wo_l, bo_l, g1, be1, wqkv_g, bqkv_g, out):
                 for f, a in todo:
                     f(a)
                 todo = []
-                if (r >= 0 or s == TURN_STEP) and turn_i % TURN_PAIR == 0:
-                    for i in range(turn_i, turn_i + TURN_PAIR):
+                turned = [turn_i] if r < 0 else range(turn_i, turn_i + TURN_PAIR) if r % TURN_PAIR == 0 else []
+                if r >= 0 or s == TURN_STEP:
+                    for i in turned:
                         if live(i):
                             turn(i)
                             todo.append((quantise_local, i))
-                if r < 0:
-                    n = UNITS_A_ROUND * (r - FIRST_ROUND) + s
-                    w = WO_UNITS + n
+                n = UNITS_A_ROUND * (r - FIRST_ROUND) + s if r < 0 else UNITS_A_ROUND * -FIRST_ROUND + r
+                w = WO_UNITS + n
+                if w < len(units):
                     transpose_unit_half(w, 0, False)
-                    transpose_unit_half(w, 1, s in WV)
+                    transpose_unit_half(w, 1, (s in WV and r < 0) or (not live(n + P_LEAD) and WV_IDLE and r < 0))
                     todo.append((quantise_unit, w))
+                if r < 0:
                     if live(n + X_EARLY):
                         transpose_tokens(n + X_EARLY, False)
                         todo.append((quantise_tokens, n + X_EARLY))
                     if live(n + P_LEAD):
                         project(n + P_LEAD)
-                if live(norm_i) and (r >= 0 or s == (UNITS_A_ROUND - 1 if r == FIRST_ROUND else NORM_STEP)):
+                if live(norm_i) and (r >= 0 or s == NORM_STEP):
                     normalise(norm_i)
             if live(r):
-                qkv(r)
+                qkv(products(r), todo)
+                if Q_POS < OUT_CHUNKS:
+                    todo = []

@@ -31,7 +31,7 @@ WO_UNITS = WO_CHUNKS * PASSES
 
 NORM_AHEAD = 4
 TURN_AHEAD = 2
-TURN_PAIR = 1
+PAIR_FROM = 99
 UNITS_A_ROUND = 2
 LATE_FIRST = False
 FIRST_ROUND = -5
@@ -53,7 +53,10 @@ WV = (0,)
 WO_V = (1, 3)
 XH_V = (1,)
 OG = ()
-NORM_G = True
+MEAN_G = True
+MEAN_BUFS = 8
+SQ_FIRST = True
+RSTD_POS = 1
 XORD = [[0, 1], [2], [3], [4], [], []]
 OG_ADD_LATE = 1
 
@@ -247,30 +250,36 @@ def tile_hlgan_pb_kernel(tc, attn_l, wo_l, bo_l, g1, be1, wqkv_g, bqkv_g, out):
             y[i] = y_tile
             y_sum[i] = sums
 
-        def normalise(i):
-            scaled = small.tile([P, WO_CHUNKS], F32, tag="scaled")
-            neg_mean = small.tile([P, 1], F32, tag="neg_mean")
-            nc.scalar.activation(
-                out=scaled[:], in_=y_sum[i][:], func=ACT.Copy, scale=-1.0 / D, accum_out=neg_mean[:]
+        def mean_step(i):
+            result = small.tile([P, 1], F32, tag="neg_mean", bufs=MEAN_BUFS)
+            eng = nc.gpsimd if MEAN_G else nc.vector
+            eng.tensor_scalar(
+                out=result[:],
+                in0=y_sum[i][:, 0:1],
+                scalar1=y_sum[i][:, 1:2],
+                scalar2=-1.0 / D,
+                op0=ALU.add,
+                op1=ALU.mult,
             )
+            neg_mean[i] = result
+
+        def squares_step(i):
             squares = norm.tile([P, D], BF16, tag="squares", bufs=1)
-            sum_sq = small.tile([P, 1], F32, tag="sum_sq")
+            result = small.tile([P, 1], F32, tag="sum_sq")
             nc.scalar.activation(
-                out=squares[:], in_=y[i][:], func=ACT.Square, bias=neg_mean[:], accum_out=sum_sq[:]
+                out=squares[:], in_=y[i][:], func=ACT.Square, bias=neg_mean[i][:], accum_out=result[:]
             )
+            sum_sq[i] = result
+
+        def normalise_step(i):
             rstd = small.tile([P, 1], F32, tag="rstd")
             nc.scalar.activation(
-                out=rstd[:], in_=sum_sq[:], func=ACT.Abs_reciprocal_sqrt, bias=eps[:], scale=1.0 / D
+                out=rstd[:], in_=sum_sq[i][:], func=ACT.Abs_reciprocal_sqrt, bias=eps[:], scale=1.0 / D
             )
-            offset = small.tile([P, 1], F32, tag="offset")
-            nc.scalar.mul(out=offset[:], in_=neg_mean[:], mul=rstd[:])
             result = norm.tile([P, D], F32, tag="z", bufs=Z_BUFS)
-            if NORM_G:
-                nc.gpsimd.tensor_scalar(
-                    out=result[:], in0=y[i][:], scalar1=rstd[:], scalar2=offset[:], op0=ALU.mult, op1=ALU.add
-                )
-            else:
-                nc.scalar.activation(out=result[:], in_=y[i][:], func=ACT.Identity, bias=offset[:], scale=rstd[:])
+            nc.gpsimd.tensor_scalar(
+                out=result[:], in0=y[i][:], scalar1=neg_mean[i][:], scalar2=rstd[:], op0=ALU.add, op1=ALU.mult
+            )
             z[i] = result
 
         def turn(i):
@@ -374,34 +383,44 @@ def tile_hlgan_pb_kernel(tc, attn_l, wo_l, bo_l, g1, be1, wqkv_g, bqkv_g, out):
                 todo.append((quantise_tokens, i))
             for i in range(P_LEAD):
                 project(i)
+                todo.append((mean_step, i))
 
         for r in range(FIRST_ROUND, TOKEN_TILES):
             norm_i, turn_i = r + NORM_AHEAD, r + TURN_AHEAD
             for s in range(UNITS_A_ROUND if r < 0 else 1):
-                last = r >= 0 or s == UNITS_A_ROUND - 1
                 for f, a in todo:
                     f(a)
                 todo = []
-                turned = [turn_i] if r < 0 else range(turn_i, turn_i + TURN_PAIR) if r % TURN_PAIR == 0 else []
+                norms = live(norm_i) and (r >= 0 or s == NORM_STEP)
+                if norms and SQ_FIRST:
+                    squares_step(norm_i)
+                turned = [turn_i] if r < PAIR_FROM else range(turn_i, turn_i + 2) if (r - PAIR_FROM) % 2 == 0 else []
                 if r >= 0 or s == TURN_STEP:
                     for i in turned:
                         if live(i):
                             turn(i)
                             todo.append((quantise_local, i))
+                if norms and not SQ_FIRST:
+                    squares_step(norm_i)
                 n = UNITS_A_ROUND * (r - FIRST_ROUND) + s if r < 0 else UNITS_A_ROUND * -FIRST_ROUND + r
                 w = WO_UNITS + n
+                if norms and RSTD_POS == 0:
+                    normalise_step(norm_i)
                 if w < len(units):
                     transpose_unit_half(w, 0, False)
-                    transpose_unit_half(w, 1, (s in WV and r < 0) or (not live(n + P_LEAD) and WV_IDLE and r < 0))
+                    if norms and RSTD_POS == 1:
+                        normalise_step(norm_i)
+                    transpose_unit_half(w, 1, s in WV and r < 0)
                     todo.append((quantise_unit, w))
+                if norms and (RSTD_POS == 2 or w >= len(units) and RSTD_POS == 1):
+                    normalise_step(norm_i)
                 if r < 0:
                     if live(n + X_EARLY):
                         transpose_tokens(n + X_EARLY, False)
                         todo.append((quantise_tokens, n + X_EARLY))
                     if live(n + P_LEAD):
                         project(n + P_LEAD)
-                if live(norm_i) and (r >= 0 or s == NORM_STEP):
-                    normalise(norm_i)
+                        todo.append((mean_step, n + P_LEAD))
             if live(r):
                 qkv(products(r), todo)
                 if Q_POS < OUT_CHUNKS:

@@ -31,14 +31,14 @@ WO_UNITS = WO_CHUNKS * PASSES
 
 NORM_AHEAD = 4
 TURN_AHEAD = 2
-PAIR_FROM = 99
+PAIR_FROM = 5
 UNITS_A_ROUND = 2
 LATE_FIRST = False
-FIRST_ROUND = -5
+FIRST_ROUND = -4
 NORM_LAST_FIRST = False
 X_EARLY = 4
-P_LEAD = 1
-Q_POS = 9
+P_LEAD = 2
+Q_POS = 3
 WV_IDLE = False
 X_AFTER = 5
 HEAD = 1
@@ -47,12 +47,13 @@ NORM_STEP = 1
 W_BUFS = 5
 Y_BUFS = 8
 Z_BUFS = 4
-OUT_BUFS = 8
+OUT_BUFS = 10
 T_BANKS = 4
 WV = (0,)
 WO_V = (1, 3)
 XH_V = (1,)
 OG = ()
+JOIN = False
 MEAN_G = True
 MEAN_BUFS = 8
 SQ_FIRST = True
@@ -282,32 +283,36 @@ def tile_hlgan_pb_kernel(tc, attn_l, wo_l, bo_l, g1, be1, wqkv_g, bqkv_g, out):
             )
             z[i] = result
 
-        def turn(i):
-            tile_planes = norm.tile([P, PASSES, PACK, P], BF16, tag="planes")
-            for g in range(PASSES):
-                bank = psum_t.tile([P, PACK, P], F32, tag="tp")
-                for t in range(PACK):
-                    j = PACK * g + t
-                    nc.tensor.transpose(bank[:, t, :], z[i][:, P * j : P * (j + 1)], ident[:])
-                for t in range(PACK):
-                    j = PACK * g + t
+        def turn(tiles):
+            count = len(tiles)
+            turned = norm.tile([P, PASSES, PACK, count, P], BF16, tag="planes")
+            in_bank = ROW_TILES // count
+            for first in range(0, FEATURE_TILES, in_bank):
+                bank = psum_t.tile([P, in_bank, count, P], F32, tag="tp")
+                for b in range(in_bank):
+                    j = first + b
+                    for c in range(count):
+                        nc.tensor.transpose(bank[:, b, c, :], z[tiles[c]][:, P * j : P * (j + 1)], ident[:])
+                for b in range(in_bank):
+                    j = first + b
                     nc.scalar.activation(
-                        out=tile_planes[:, g, t, :],
-                        in_=bank[:, t, :],
+                        out=turned[:, j // PACK, j % PACK].rearrange("q c r -> q (c r)"),
+                        in_=bank[:, b].rearrange("q c r -> q (c r)"),
                         func=ACT.Identity,
                         bias=shift[:, j : j + 1],
                         scale=gain[:, j : j + 1],
                     )
-            grouped = norm.tile([P, D], BF16, align_bytes=64, tag="local_grouped")
-            nc.gpsimd.tensor_scalar(
-                out=grouped[:].rearrange("q (g r t) -> q g r t", g=PASSES, t=PACK),
-                in0=tile_planes[:].rearrange("q g t r -> q g r t"),
-                scalar1=1.0,
-                scalar2=0.0,
-                op0=ALU.mult,
-                op1=ALU.add,
-            )
-            local_grouped[i] = grouped
+            for c in range(count):
+                grouped = norm.tile([P, D], BF16, align_bytes=64, tag="local_grouped")
+                nc.gpsimd.tensor_scalar(
+                    out=grouped[:].rearrange("q (g r t) -> q g r t", g=PASSES, t=PACK),
+                    in0=turned[:, :, :, c, :].rearrange("q g t r -> q g r t"),
+                    scalar1=1.0,
+                    scalar2=0.0,
+                    op0=ALU.mult,
+                    op1=ALU.add,
+                )
+                local_grouped[tiles[c]] = grouped
 
         early_units = UNITS_A_ROUND * -FIRST_ROUND
 
@@ -385,21 +390,27 @@ def tile_hlgan_pb_kernel(tc, attn_l, wo_l, bo_l, g1, be1, wqkv_g, bqkv_g, out):
                 project(i)
                 todo.append((mean_step, i))
 
+        later = {}
+        pending = []
         for r in range(FIRST_ROUND, TOKEN_TILES):
             norm_i, turn_i = r + NORM_AHEAD, r + TURN_AHEAD
             for s in range(UNITS_A_ROUND if r < 0 else 1):
-                for f, a in todo:
-                    f(a)
-                todo = []
+                if not JOIN or s == 0:
+                    for f, a in todo:
+                        f(a)
+                    todo = []
                 norms = live(norm_i) and (r >= 0 or s == NORM_STEP)
                 if norms and SQ_FIRST:
                     squares_step(norm_i)
                 turned = [turn_i] if r < PAIR_FROM else range(turn_i, turn_i + 2) if (r - PAIR_FROM) % 2 == 0 else []
                 if r >= 0 or s == TURN_STEP:
-                    for i in turned:
-                        if live(i):
-                            turn(i)
-                            todo.append((quantise_local, i))
+                    turned = [i for i in turned if live(i)]
+                    if turned:
+                        turn(turned)
+                    if r < PAIR_FROM:
+                        todo.extend((quantise_local, i) for i in turned)
+                    else:
+                        later[r + 1] = [(quantise_local, i) for i in turned]
                 if norms and not SQ_FIRST:
                     squares_step(norm_i)
                 n = UNITS_A_ROUND * (r - FIRST_ROUND) + s if r < 0 else UNITS_A_ROUND * -FIRST_ROUND + r
@@ -419,9 +430,11 @@ def tile_hlgan_pb_kernel(tc, attn_l, wo_l, bo_l, g1, be1, wqkv_g, bqkv_g, out):
                         transpose_tokens(n + X_EARLY, False)
                         todo.append((quantise_tokens, n + X_EARLY))
                     if live(n + P_LEAD):
-                        project(n + P_LEAD)
-                        todo.append((mean_step, n + P_LEAD))
+                        pending.append(n + P_LEAD)
+                    if not JOIN or s == UNITS_A_ROUND - 1:
+                        for i in pending:
+                            project(i)
+                            todo.append((mean_step, i))
+                        pending = []
             if live(r):
-                qkv(products(r), todo)
-                if Q_POS < OUT_CHUNKS:
-                    todo = []
+                qkv(products(r), later.get(r, []))

from contextlib import ExitStack

import concourse.mybir as mybir
from concourse.masks import make_identity

F32 = mybir.dt.float32
BF16 = mybir.dt.bfloat16
I32 = mybir.dt.int32
U32 = mybir.dt.uint32
U8 = mybir.dt.uint8
FP8X4 = mybir.dt.float8_e4m3fn_x4
ALU = mybir.AluOpType
ACT = mybir.ActivationFunctionType

P = 128
TOKEN_TILES = 10
D = 1024
D3 = 3072
EPS = 1e-5
PACK = 4
K_PASS = P * PACK
PASSES = D // K_PASS
PAIRS = 2
WORDS_PER_PASS = K_PASS // PAIRS
CHUNK = 512
ROW_TILES = CHUNK // P
FEATURE_TILES = D // P
WO_CHUNKS = D // CHUNK
OUT_CHUNKS = D3 // CHUNK
WO_UNITS = WO_CHUNKS * PASSES

NORM_AHEAD = 4
TURN_AHEAD = 2
PAIR_FROM = 5
UNITS_A_ROUND = 2
LATE_FIRST = False
FIRST_ROUND = -4
NORM_LAST_FIRST = False
X_EARLY = 4
P_LEAD = 2
Q_POS = 3
WV_IDLE = False
X_AFTER = 5
HEAD = 1
TURN_STEP = 0
NORM_STEP = 1
W_BUFS = 5
Y_BUFS = 8
Z_BUFS = 4
OUT_BUFS = 10
T_BANKS = 4
WV = (0,)
WO_V = (1, 3)
XH_V = (1,)
OG = ()
JOIN = False
MEAN_G = True
MEAN_BUFS = 8
SQ_FIRST = True
RSTD_POS = 1
XORD = [[0, 1], [2], [3], [4], [], []]
OG_ADD_LATE = 1

FLOPS = 2 * P * TOKEN_TILES * D * (D + D3)


def tile_hlgan_pb_kernel(tc, attn_l, wo_l, bo_l, g1, be1, wqkv_g, bqkv_g, out):
    nc = tc.nc
    with ExitStack() as ctx:
        const = ctx.enter_context(tc.tile_pool(name="const", bufs=1))
        keep = ctx.enter_context(tc.tile_pool(name="keep", bufs=1))
        stage = ctx.enter_context(tc.tile_pool(name="stage", bufs=2))
        norm = ctx.enter_context(tc.tile_pool(name="norm", bufs=2))
        small = ctx.enter_context(tc.tile_pool(name="small", bufs=2))
        out_pool = ctx.enter_context(tc.tile_pool(name="out_pool", bufs=OUT_BUFS))
        psum_t = ctx.enter_context(tc.psum_pool(name="psum_t", bufs=T_BANKS))
        psum_acc = ctx.enter_context(tc.psum_pool(name="psum_acc", bufs=8 - T_BANKS))
        ctx.enter_context(tc.manual_schedule())

        w_rows = []
        wo_view = wo_l.rearrange("(a q e) k -> q a e k", q=P, e=PAIRS)
        x_raw = keep.tile([P, TOKEN_TILES, D], BF16)
        for h in range(WO_CHUNKS):
            if h == X_AFTER:
                nc.sync.dma_start(out=x_raw[:, 0:2, :], in_=attn_l[:, 0:2, :])
            rows = stage.tile([P, ROW_TILES, D], BF16, tag="w_rows", bufs=W_BUFS)
            for a in range(ROW_TILES // PAIRS):
                nc.sync.dma_start(
                    out=rows[:, PAIRS * a : PAIRS * (a + 1)], in_=wo_view[:, ROW_TILES // PAIRS * h + a]
                )
            w_rows.append(rows)
        bo_row = const.tile([P, D], BF16)
        nc.vector.memset(bo_row[:].bitcast(I32), 0)
        nc.sync.dma_start(out=bo_row[0:1, :], in_=bo_l.unsqueeze(0))
        g_raw = const.tile([P, FEATURE_TILES], BF16)
        be_raw = const.tile([P, FEATURE_TILES], BF16)
        for n in range(OUT_CHUNKS):
            for m in XORD[n]:
                if m == 0 and X_AFTER == 1:
                    continue
                nc.sync.dma_start(out=x_raw[:, 2 * m : 2 * m + 2, :], in_=attn_l[:, 2 * m : 2 * m + 2, :])
            rows = stage.tile([P, ROW_TILES, D], BF16, tag="w_rows", bufs=W_BUFS)
            nc.sync.dma_start(
                out=rows[:], in_=wqkv_g[CHUNK * n : CHUNK * (n + 1), :].rearrange("(j p) k -> p j k", p=P)
            )
            w_rows.append(rows)
            if n == 0:
                nc.sync.dma_start(
                    out=g_raw[:].rearrange("q (a e) -> q a e", e=PAIRS),
                    in_=g1.rearrange("(a q e) -> q a e", q=P, e=PAIRS),
                )
                nc.sync.dma_start(
                    out=be_raw[:].rearrange("q (a e) -> q a e", e=PAIRS),
                    in_=be1.rearrange("(a q e) -> q a e", q=P, e=PAIRS),
                )
        bqkv_rows = const.tile([P, D3], BF16)
        nc.sync.dma_start(out=bqkv_rows[:], in_=bqkv_g.partition_broadcast(P))

        ident = const.tile([P, P], F32)
        make_identity(nc, ident[:])
        ones = const.tile([P, P], BF16)
        nc.vector.memset(ones[:], 1.0)
        eps = const.tile([P, 1], F32)
        nc.vector.memset(eps[:], EPS)
        warm = const.tile([P, 1], F32)
        nc.scalar.activation(out=warm[:], in_=eps[:], func=ACT.Abs_reciprocal_sqrt)
        gain = const.tile([P, FEATURE_TILES], F32)
        nc.gpsimd.tensor_copy(out=gain[:], in_=g_raw[:])
        shift = const.tile([P, FEATURE_TILES], F32)
        nc.gpsimd.tensor_copy(out=shift[:], in_=be_raw[:])
        bo_cols = const.tile([P, D], BF16)

        x_codes = keep.tile([P, TOKEN_TILES, PASSES, P], U32, align_bytes=256)
        x_scales = keep.tile([P, TOKEN_TILES, PASSES, P], U8, align_bytes=256)
        wo_codes = keep.tile([P, PASSES, D], U32, align_bytes=256)
        wo_scales = keep.tile([P, PASSES, D], U8, align_bytes=256)
        local_codes = keep.tile([P, TOKEN_TILES, PASSES, P], U32, align_bytes=256)
        local_scales = keep.tile([P, TOKEN_TILES, PASSES, P], U8, align_bytes=256)
        wqkv_codes = keep.tile([P, PASSES, D3], U32, align_bytes=256)
        wqkv_scales = keep.tile([P, PASSES, D3], U8, align_bytes=256)

        units = []
        for n in range(WO_CHUNKS + OUT_CHUNKS):
            if n < WO_CHUNKS:
                codes, scales, first_col = wo_codes, wo_scales, CHUNK * n
            else:
                codes, scales, first_col = wqkv_codes, wqkv_scales, CHUNK * (n - WO_CHUNKS)
            cols = slice(first_col, first_col + CHUNK)
            rows = [w_rows[n][:, j, :].bitcast(F32) for j in range(ROW_TILES)]
            for g in range(PASSES):
                units.append((rows, g, codes[:, g, cols], scales[:, g, cols]))

        def live(i):
            return 0 <= i < TOKEN_TILES

        def copy_out(dst, src, on_vector):
            if on_vector:
                nc.vector.tensor_copy(out=dst, in_=src)
            else:
                nc.scalar.copy(out=dst, in_=src)

        w_grouped, x_grouped, y, y_sum, neg_mean, sum_sq = {}, {}, {}, {}, {}, {}
        rstd, neg_mean_rstd, z, planes, local_grouped = {}, {}, {}, {}, {}

        def transpose_unit_half(w, half, on_vector):
            rows, g = units[w][0], units[w][1]
            if half == 0:
                grouped = stage.tile([P, PACK * CHUNK], BF16, align_bytes=64, tag="w_grouped", bufs=3)
                w_grouped[w] = grouped
            bank = psum_t.tile([P, PAIRS, 2, P], F32, tag="tp")
            for u in range(PAIRS):
                first = WORDS_PER_PASS * g + P * u
                for j in range(2):
                    nc.tensor.transpose(bank[:, u, j, :], rows[2 * half + j][:, first : first + P], ident[:])
            words = w_grouped[w][:].bitcast(F32).rearrange("q (n u) -> q n u", u=PAIRS)
            copy_out(
                words[:, 2 * P * half : 2 * P * (half + 1), :],
                bank[:].rearrange("q u j r -> q (j r) u"),
                on_vector,
            )

        def transpose_tokens(i, on_vector):
            x_words = x_raw[:, i, :].bitcast(F32)
            bank = psum_t.tile([P, PASSES, PAIRS, P], F32, tag="tp")
            for g in range(PASSES):
                for u in range(PAIRS):
                    first = WORDS_PER_PASS * g + P * u
                    nc.tensor.transpose(bank[:, g, u, :], x_words[:, first : first + P], ident[:])
            grouped = stage.tile([P, D], BF16, align_bytes=64, tag="x_grouped")
            copy_out(
                grouped[:].bitcast(F32).rearrange("q (g r u) -> q g r u", g=PASSES, u=PAIRS),
                bank[:].rearrange("q g u r -> q g r u"),
                on_vector,
            )
            x_grouped[i] = grouped

        def spread_bias():
            for h in range(WO_CHUNKS):
                cols = slice(CHUNK * h, CHUNK * (h + 1))
                acc = psum_acc.tile([P, CHUNK], F32, tag="acc")
                nc.tensor.matmul(out=acc[:], lhsT=ones[:], rhs=bo_row[:, cols], start=True, stop=True)
                nc.scalar.copy(
                    out=bo_cols[:, cols].rearrange("p (a e q) -> p a e q", e=PAIRS, q=P),
                    in_=acc[:].rearrange("p (a q e) -> p a e q", q=P, e=PAIRS),
                )

        def quantise_unit(w):
            nc.vector.quantize_mx(out=units[w][2].bitcast(FP8X4), scales=units[w][3], in_=w_grouped[w][:])

        def quantise_tile(grouped, codes, scales, i):
            nc.vector.quantize_mx(
                out=codes[:, i].rearrange("q g r -> q (g r)").bitcast(FP8X4),
                scales=scales[:, i].rearrange("q g r -> q (g r)"),
                in_=grouped[:],
            )

        def quantise_tokens(i):
            quantise_tile(x_grouped[i], x_codes, x_scales, i)

        def quantise_local(i):
            quantise_tile(local_grouped[i], local_codes, local_scales, i)

        def multiply(acc, a_codes, a_scales, i, b_codes, b_scales, cols):
            for g in range(PASSES):
                nc.tensor.matmul_mx(
                    out=acc[:],
                    lhsT=a_codes[:, i, g, :].bitcast(FP8X4),
                    lhsT_scale=a_scales[:, i, g, :],
                    rhs=b_codes[:, g, cols].bitcast(FP8X4),
                    rhs_scale=b_scales[:, g, cols],
                    start=(g == 0),
                    stop=(g == PASSES - 1),
                )

        def project(i):
            y_tile = norm.tile([P, D], F32, tag="y", bufs=Y_BUFS)
            sums = small.tile([P, WO_CHUNKS], F32, tag="y_sum", bufs=Y_BUFS)
            for h in range(WO_CHUNKS):
                cols = slice(CHUNK * h, CHUNK * (h + 1))
                acc = psum_acc.tile([P, CHUNK], F32, tag="acc")
                multiply(acc, x_codes, x_scales, i, wo_codes, wo_scales, cols)
                nc.vector.scalar_tensor_tensor(
                    out=y_tile[:, cols],
                    in0=acc[:],
                    scalar=0.0,
                    in1=bo_cols[:, cols],
                    op0=ALU.add,
                    op1=ALU.add,
                    accum_out=sums[:, h : h + 1],
                )
            y[i] = y_tile
            y_sum[i] = sums

        def mean_step(i):
            result = small.tile([P, 1], F32, tag="neg_mean", bufs=MEAN_BUFS)
            eng = nc.gpsimd if MEAN_G else nc.vector
            eng.tensor_scalar(
                out=result[:],
                in0=y_sum[i][:, 0:1],
                scalar1=y_sum[i][:, 1:2],
                scalar2=-1.0 / D,
                op0=ALU.add,
                op1=ALU.mult,
            )
            neg_mean[i] = result

        def squares_step(i):
            squares = norm.tile([P, D], BF16, tag="squares", bufs=1)
            result = small.tile([P, 1], F32, tag="sum_sq")
            nc.scalar.activation(
                out=squares[:], in_=y[i][:], func=ACT.Square, bias=neg_mean[i][:], accum_out=result[:]
            )
            sum_sq[i] = result

        def normalise_step(i):
            rstd = small.tile([P, 1], F32, tag="rstd")
            nc.scalar.activation(
                out=rstd[:], in_=sum_sq[i][:], func=ACT.Abs_reciprocal_sqrt, bias=eps[:], scale=1.0 / D
            )
            result = norm.tile([P, D], F32, tag="z", bufs=Z_BUFS)
            nc.gpsimd.tensor_scalar(
                out=result[:], in0=y[i][:], scalar1=neg_mean[i][:], scalar2=rstd[:], op0=ALU.add, op1=ALU.mult
            )
            z[i] = result

        def turn(tiles):
            count = len(tiles)
            turned = norm.tile([P, PASSES, PACK, count, P], BF16, tag="planes")
            in_bank = ROW_TILES // count
            for first in range(0, FEATURE_TILES, in_bank):
                bank = psum_t.tile([P, in_bank, count, P], F32, tag="tp")
                for b in range(in_bank):
                    j = first + b
                    for c in range(count):
                        nc.tensor.transpose(bank[:, b, c, :], z[tiles[c]][:, P * j : P * (j + 1)], ident[:])
                for b in range(in_bank):
                    j = first + b
                    nc.scalar.activation(
                        out=turned[:, j // PACK, j % PACK].rearrange("q c r -> q (c r)"),
                        in_=bank[:, b].rearrange("q c r -> q (c r)"),
                        func=ACT.Identity,
                        bias=shift[:, j : j + 1],
                        scale=gain[:, j : j + 1],
                    )
            for c in range(count):
                grouped = norm.tile([P, D], BF16, align_bytes=64, tag="local_grouped")
                nc.gpsimd.tensor_scalar(
                    out=grouped[:].rearrange("q (g r t) -> q g r t", g=PASSES, t=PACK),
                    in0=turned[:, :, :, c, :].rearrange("q g t r -> q g r t"),
                    scalar1=1.0,
                    scalar2=0.0,
                    op0=ALU.mult,
                    op1=ALU.add,
                )
                local_grouped[tiles[c]] = grouped

        early_units = UNITS_A_ROUND * -FIRST_ROUND

        def ready_round(n):
            return max(0, PASSES * (n + 1) - early_units)

        def products(r):
            late = [(i, n) for n in range(OUT_CHUNKS) if 0 < ready_round(n) == r for i in range(r)]
            own = [(r, n) for n in range(OUT_CHUNKS) if ready_round(n) <= r]
            return late + own if LATE_FIRST else own + late

        def qkv(pairs, after):
            for count, (i, n) in enumerate(pairs):
                if count == Q_POS:
                    for f, a in after:
                        f(a)
                cols = slice(CHUNK * n, CHUNK * (n + 1))
                acc = psum_acc.tile([P, CHUNK], F32, tag="acc")
                multiply(acc, local_codes, local_scales, i, wqkv_codes, wqkv_scales, cols)
                result = out_pool.tile([P, CHUNK], F32, tag="result")
                if n in OG and i < TOKEN_TILES - 1:
                    raw = out_pool.tile([P, CHUNK], F32, tag="raw", bufs=2)
                    nc.scalar.copy(out=raw[:], in_=acc[:])
                    nc.gpsimd.tensor_tensor(out=result[:], in0=raw[:], in1=bqkv_rows[:, cols], op=ALU.add)
                else:
                    nc.vector.tensor_tensor(out=result[:], in0=acc[:], in1=bqkv_rows[:, cols], op=ALU.add)
                nc.sync.dma_start(out=out[:, i, cols], in_=result[:])

        def unit_pair(h):
            for half in range(2):
                for g in range(PASSES):
                    transpose_unit_half(PASSES * h + g, half, 4 * h + 2 * half + g in WO_V)

        if HEAD == 0:
            unit_pair(0)
            for i in range(2):
                transpose_tokens(i, i in XH_V)
            quantise_unit(0)
            quantise_unit(1)
            spread_bias()
            quantise_tokens(0)
            quantise_tokens(1)
            unit_pair(1)
            quantise_unit(2)
            quantise_unit(3)
            todo = []
            for i in range(2, X_EARLY):
                transpose_tokens(i, i in XH_V)
                todo.append((quantise_tokens, i))
            for i in range(P_LEAD):
                project(i)
        else:
            unit_pair(0)
            quantise_unit(0)
            quantise_unit(1)
            unit_pair(1)
            for i in range(2):
                transpose_tokens(i, i in XH_V)
            spread_bias()
            if HEAD == 1:
                quantise_tokens(0)
                quantise_unit(2)
                quantise_unit(3)
                quantise_tokens(1)
            else:
                quantise_unit(2)
                quantise_unit(3)
                quantise_tokens(0)
                quantise_tokens(1)
            todo = []
            for i in range(2, X_EARLY):
                transpose_tokens(i, i in XH_V)
                todo.append((quantise_tokens, i))
            for i in range(P_LEAD):
                project(i)
                todo.append((mean_step, i))

        later = {}
        pending = []
        for r in range(FIRST_ROUND, TOKEN_TILES):
            norm_i, turn_i = r + NORM_AHEAD, r + TURN_AHEAD
            for s in range(UNITS_A_ROUND if r < 0 else 1):
                if not JOIN or s == 0:
                    for f, a in todo:
                        f(a)
                    todo = []
                norms = live(norm_i) and (r >= 0 or s == NORM_STEP)
                if norms and SQ_FIRST:
                    squares_step(norm_i)
                turned = [turn_i] if r < PAIR_FROM else range(turn_i, turn_i + 2) if (r - PAIR_FROM) % 2 == 0 else []
                if r >= 0 or s == TURN_STEP:
                    turned = [i for i in turned if live(i)]
                    if turned:
                        turn(turned)
                    if r < PAIR_FROM:
                        todo.extend((quantise_local, i) for i in turned)
                    else:
                        later[r + 1] = [(quantise_local, i) for i in turned]
                if norms and not SQ_FIRST:
                    squares_step(norm_i)
                n = UNITS_A_ROUND * (r - FIRST_ROUND) + s if r < 0 else UNITS_A_ROUND * -FIRST_ROUND + r
                w = WO_UNITS + n
                if norms and RSTD_POS == 0:
                    normalise_step(norm_i)
                if w < len(units):
                    transpose_unit_half(w, 0, False)
                    if norms and RSTD_POS == 1:
                        normalise_step(norm_i)
                    transpose_unit_half(w, 1, s in WV and r < 0)
                    todo.append((quantise_unit, w))
                if norms and (RSTD_POS == 2 or w >= len(units) and RSTD_POS == 1):
                    normalise_step(norm_i)
                if r < 0:
                    if live(n + X_EARLY):
                        transpose_tokens(n + X_EARLY, False)
                        todo.append((quantise_tokens, n + X_EARLY))
                    if live(n + P_LEAD):
                        pending.append(n + P_LEAD)
                    if not JOIN or s == UNITS_A_ROUND - 1:
                        for i in pending:
                            project(i)
                            todo.append((mean_step, i))
                        pending = []
            if live(r):
                qkv(products(r), later.get(r, []))
